import numpy as np
import ml_dtypes


def mxq(x, axis, fmt="e4m3"):
    dtype, down = {"e4m3": (ml_dtypes.float8_e4m3fn, 7), "e5m2": (ml_dtypes.float8_e5m2, 14)}[fmt]
    v = np.moveaxis(np.asarray(x, np.float32).astype(ml_dtypes.bfloat16).astype(np.float64), axis, -1)
    blocks = v.reshape(v.shape[:-1] + (-1, 32))
    amax = np.abs(blocks).max(-1, keepdims=True)
    byte = np.maximum(np.where(amax > 0, np.frexp(amax)[1] - 1 + 127, 0) - down, 1)
    scale = np.exp2(byte - 127.0)
    codes = (blocks / scale).astype(np.float32).astype(dtype).astype(np.float64)
    return np.moveaxis((codes * scale).reshape(v.shape), -1, axis)


WIDE = False


def mx_kscale(k):
    if not WIDE:
        return np.ones(k)
    levels = np.array([10, -10, 5, -5, 0])
    a = np.random.permutation(np.resize(levels, k // 512 * 4)).reshape(k // 512, 4)
    idx = np.arange(k)
    return np.exp2(a[idx // 512, idx % 128 // 32])


BF16 = ml_dtypes.bfloat16


def bf(x):
    return np.asarray(x, np.float32).astype(BF16)


def f64(x):
    return np.asarray(x).astype(np.float64)


B, P, D, NL, T, E, G = 2, 192, 1024, 16, 2, 1, 2
WW = NL * NL * T
WG = WW * G
CLIP = 1.0
LOG_2PI = np.log(2.0 * np.pi)


def clip(v):
    return np.clip(v, -CLIP, CLIP)


def gaussian_scale(m1, v1, m2, v2):
    add = np.exp(2.0 * v1) + np.exp(2.0 * v2)
    return (-0.5 * (LOG_2PI + np.log(add) + (m1 - m2) ** 2 / add)).sum(-1)


def setup_inputs():
    s = mx_kscale(D)
    return {"x_next": bf(np.random.standard_normal((B, P, D)) * s),
            "cs_scale": bf(np.random.standard_normal((B, P, NL, NL, T, E)) * 1.2 - 3.4),
            "cs_mu": bf(clip(np.random.standard_normal((B, P, NL, NL, T, E, G)) * 0.55)),
            "cs_var": bf(np.random.standard_normal((B, P, NL, NL, T, E, G)) * 0.5 - 0.5),
            "mask_here": bf(0.5 + np.random.random((B, P))),
            "mask_next": bf(0.5 + np.random.random((B, P))),
            "tw_w": bf(np.random.standard_normal((D, WW)) / np.sqrt(D) / s[:, None]),
            "tw_b": bf(np.random.standard_normal(WW) * 0.3),
            "tpm_w": bf(np.random.standard_normal((D, WG)) / np.sqrt(D) / s[:, None]),
            "tpm_b": bf(np.random.standard_normal(WG) * 0.3),
            "tpv_w": bf(np.random.standard_normal((D, WG)) / np.sqrt(D) / s[:, None]),
            "tpv_b": bf(np.random.standard_normal(WG) * 0.3)}


def reference(x_next, cs_scale, cs_mu, cs_var, mask_here, mask_next, tw_w, tw_b, tpm_w, tpm_b, tpv_w, tpv_b):
    xq = mxq(f64(x_next).reshape(B * P, D), 1, "e4m3")
    t_weight = ((xq @ mxq(f64(tw_w), 0, "e4m3")) + f64(tw_b)).reshape(B, P, NL, NL, T)[:, :, None, :, :, None, None, :]
    t_p_mu = clip(((xq @ mxq(f64(tpm_w), 0, "e4m3")) + f64(tpm_b)).reshape(B, P, NL, NL, T, G))[:, :, None, :, :, None, None, :, :]
    t_p_var = clip(((xq @ mxq(f64(tpv_w), 0, "e4m3")) + f64(tpv_b)).reshape(B, P, NL, NL, T, G))[:, :, None, :, :, None, None, :, :]
    a_mu = f64(cs_mu)[:, :, :, :, None, :, :, None, :]
    a_var = f64(cs_var)[:, :, :, :, None, :, :, None, :]
    m_next = f64(mask_next)[:, :, None, None, None, None, None, None]
    m_here = f64(mask_here)[:, :, None, None, None, None, None, None]
    csp_scale = gaussian_scale(a_mu, a_var, t_p_mu, t_p_var)
    csp_scale = csp_scale * m_next + f64(cs_scale)[:, :, :, :, None, :, :, None] + t_weight * m_next
    return csp_scale * m_here

@@ -1,0 +1,378 @@
+import math
+from contextlib import ExitStack
+
+import concourse.mybir as mybir
+from concourse.masks import make_identity
+
+F32 = mybir.dt.float32
+BF16 = mybir.dt.bfloat16
+U32 = mybir.dt.uint32
+U8 = mybir.dt.uint8
+FP8X4 = mybir.dt.float8_e4m3fn_x4
+ALU = mybir.AluOpType
+FUNC = mybir.ActivationFunctionType
+
+P = 128
+ROWS = 384
+ROW_TILES = ROWS // P
+D = 1024
+PACK = 4
+K_PASS = P * PACK
+PASSES = D // K_PASS
+NL = 16
+T = 2
+G = 2
+KU = NL * T
+JKU = NL * KU
+CS = NL * NL * T * G
+GRID = NL * NL * T * T
+PIECE = 512
+LOG_2PI = math.log(2.0 * math.pi)
+CHUNKS = ROW_TILES * NL
+LN_BLOCK = 8
+FINAL_LAG = LN_BLOCK + 1
+
+FLOPS = 2 * ROWS * D * (JKU + 2 * JKU * G)
+
+
+def tile_chainlveg_pb_kernel(
+    tc, x_next, cs_scale, cs_mu, cs_var, mask_here, mask_next, tw_w, tw_b, tpm_w, tpm_b, tpv_w, tpv_b, out
+):
+    nc = tc.nc
+    weights = {"tpv": tpv_w, "tpm": tpm_w, "tw": tw_w}
+    widths = {"tpv": JKU * G, "tpm": JKU * G, "tw": JKU}
+
+    x_rows = x_next.rearrange("b q k -> (b q) k").rearrange("(r p) k -> p r k", p=P)
+    var_rows = cs_var.rearrange("b q i j t e g -> (b q) (i j t e g)").rearrange("(r p) f -> p r f", p=P)
+    mu_rows = cs_mu.rearrange("b q i j t e g -> (b q) (i j t e g)").rearrange("(r p) f -> p r f", p=P)
+    scale_rows = cs_scale.rearrange("b q i j t e -> (b q) (i j t e)").rearrange("(r p) f -> p r f", p=P)
+    out_rows = out.rearrange("b q i j k t e u -> (b q) i (j k t e u)")
+
+    with ExitStack() as ctx:
+        ctx.enter_context(tc.manual_schedule())
+        keep = ctx.enter_context(tc.tile_pool(name="keep", bufs=1))
+
+        ident = keep.tile([P, P], F32, name="ident")
+        e1 = keep.tile([P, ROW_TILES, CS], F32, name="e1")
+        m1 = keep.tile([P, ROW_TILES, CS], F32, name="m1")
+        e2 = keep.tile([P, ROW_TILES, G, JKU], F32, name="e2")
+        a_term = keep.tile([P, ROW_TILES, NL * T * NL], F32, name="a_term")
+        b_term = keep.tile([P, ROW_TILES, JKU], F32, name="b_term")
+        m2_cols = keep.tile([P, JKU * G // P, ROWS], F32, name="m2_cols")
+        small = keep.tile([P, 32], F32, name="small")
+        tw_bias = keep.tile([P, 4], F32, name="tw_bias")
+        v_bias2 = keep.tile([P, 8], F32, name="v_bias2")
+        c_pos = keep.tile([P, ROW_TILES], F32, name="c_pos")
+        c_neg = keep.tile([P, ROW_TILES], F32, name="c_neg")
+        m_bias = small[:, 4:12]
+        mask_h = small[:, 20:23]
+        mask_n = small[:, 23:26]
+
+        make_identity(nc, ident[:])
+
+        with ExitStack() as pro:
+            load = pro.enter_context(tc.tile_pool(name="load", bufs=1))
+            group = pro.enter_context(tc.tile_pool(name="group", bufs=3))
+            quant = pro.enter_context(tc.tile_pool(name="quant", bufs=1))
+            psum = pro.enter_context(tc.psum_pool(name="psum", bufs=2))
+
+            rows_bf = load.tile([P, P], BF16, name="rows_bf")
+            nc.vector.memset(rows_bf[:], 0.0)
+            nc.scalar.dma_start(out=rows_bf[0:4, :], in_=tw_b.rearrange("(r p) -> r p", p=P))
+            nc.scalar.dma_start(out=rows_bf[4:12, :], in_=tpm_b.rearrange("(r p) -> r p", p=P))
+            nc.scalar.dma_start(out=rows_bf[12:20, :], in_=tpv_b.rearrange("(r p) -> r p", p=P))
+            nc.scalar.dma_start(
+                out=rows_bf[20:23, :], in_=mask_here.rearrange("b q -> (b q)").rearrange("(r p) -> r p", p=P)
+            )
+            nc.scalar.dma_start(
+                out=rows_bf[23:26, :], in_=mask_next.rearrange("b q -> (b q)").rearrange("(r p) -> r p", p=P)
+            )
+
+            x_sb = load.tile([P, ROW_TILES, D], BF16, name="x_sb")
+            nc.sync.dma_start(out=x_sb[:], in_=x_rows)
+            raw = {}
+            for name in ("tpv", "tpm", "tw"):
+                raw[name] = load.tile([P, PASSES, PACK * widths[name]], BF16, name="raw_" + name)
+            var_sb = load.tile([P, ROW_TILES, CS], BF16, name="var_sb")
+            mu_sb = load.tile([P, ROW_TILES, CS], BF16, name="mu_sb")
+            scale_sb = load.tile([P, ROW_TILES, CS // G], BF16, name="scale_sb")
+
+            def load_weight(name):
+                view = weights[name].rearrange("(c u p e) n -> c p u (e n)", c=PASSES, u=2, p=P, e=2)
+                for c in range(PASSES):
+                    nc.sync.dma_start(out=raw[name][:, c, :].rearrange("p (u f) -> p u f", u=2), in_=view[c])
+
+            load_weight("tpv")
+            nc.sync.dma_start(out=var_sb[:], in_=var_rows)
+            load_weight("tpm")
+            nc.sync.dma_start(out=mu_sb[:], in_=mu_rows)
+            load_weight("tw")
+            nc.sync.dma_start(out=scale_sb[:], in_=scale_rows)
+
+            rows_f = load.tile([P, P], F32, name="rows_f")
+            nc.vector.tensor_copy(out=rows_f[:], in_=rows_bf[:])
+            small_ps = psum.tile([P, P], F32, name="small_ps", bufs=1)
+            nc.tensor.transpose(small_ps[:], rows_f[:], ident[:])
+            nc.vector.tensor_copy(out=small[:], in_=small_ps[:, 0:32])
+            nc.vector.tensor_scalar_add(out=tw_bias[:], in0=small[:, 0:4], scalar1=-LOG_2PI)
+            nc.vector.tensor_scalar_mul(out=v_bias2[:], in0=small[:, 12:20], scalar1=2.0)
+            nc.vector.tensor_tensor(out=c_pos[:], in0=mask_h, in1=mask_n, op=ALU.mult)
+            nc.vector.tensor_scalar_mul(out=c_neg[:], in0=c_pos[:], scalar1=-1.0)
+
+            x_group = quant.tile([P, ROW_TILES * PASSES * P * PACK], BF16, name="x_group", align_bytes=64)
+            x_codes = quant.tile([P, ROW_TILES, PASSES, P], U32, name="x_codes", align_bytes=64)
+            x_scales = quant.tile([P, ROW_TILES, PASSES, P], U8, name="x_scales", align_bytes=64)
+            x_group_words = x_group[:].bitcast(F32).rearrange(
+                "p (r c m u) -> p r c m u", r=ROW_TILES, c=PASSES, m=P, u=2
+            )
+            for r in range(ROW_TILES):
+                x_words = x_sb[:, r, :].bitcast(F32)
+                xt = psum.tile([P, PASSES, 2, P], F32, name="xt")
+                for c in range(PASSES):
+                    for u in range(2):
+                        first = (c * 2 + u) * P
+                        nc.tensor.transpose(xt[:, c, u, :], x_words[:, first : first + P], ident[:])
+                nc.vector.tensor_copy(out=x_group_words[:, r], in_=xt[:].rearrange("p c u m -> p c m u"))
+            per_tile = PASSES * P * PACK
+            for r in range(ROW_TILES):
+                nc.vector.quantize_mx(
+                    out=x_codes[:, r].rearrange("p c m -> p (c m)").bitcast(FP8X4),
+                    scales=x_scales[:, r].rearrange("p c m -> p (c m)"),
+                    in_=x_group[:, r * per_tile : (r + 1) * per_tile],
+                )
+
+            codes = {}
+            scales = {}
+            for name in ("tpv", "tpm", "tw"):
+                codes[name] = quant.tile([P, PASSES, widths[name]], U32, name="codes_" + name, align_bytes=64)
+                scales[name] = quant.tile([P, PASSES, widths[name]], U8, name="scales_" + name, align_bytes=64)
+            units = [(name, c) for name in ("tpv", "tpm", "tw") for c in range(PASSES)]
+            grouped = {}
+            pieces_done = 0
+            for index in range(len(units) + 1):
+                if index < len(units):
+                    name, c = units[index]
+                    grouped[index] = group.tile([P, PACK * JKU * G], BF16, name="grouped", align_bytes=64)
+                    src = raw[name][:, c, :].rearrange("p (t a i) -> p a t i", t=PACK, i=4)
+                    dst = grouped[index][:, 0 : PACK * widths[name]].rearrange("p (a i t) -> p a t i", i=4, t=PACK)
+                    for h in range(widths[name] // PIECE):
+                        runs = slice(h * PIECE // 4, (h + 1) * PIECE // 4)
+                        if pieces_done % 2 == 0:
+                            nc.vector.tensor_copy(out=dst[:, runs], in_=src[:, runs])
+                        else:
+                            nc.scalar.copy(out=dst[:, runs], in_=src[:, runs])
+                        pieces_done += 1
+                if index > 0:
+                    name, c = units[index - 1]
+                    nc.vector.quantize_mx(
+                        out=codes[name][:, c, :].bitcast(FP8X4),
+                        scales=scales[name][:, c, :],
+                        in_=grouped[index - 1][:, 0 : PACK * widths[name]],
+                    )
+
+            for r in range(ROW_TILES):
+                nc.scalar.activation(out=e1[:, r, :], in_=var_sb[:, r, :], func=FUNC.Exp, scale=2.0)
+                nc.vector.tensor_copy(out=m1[:, r, :], in_=mu_sb[:, r, :])
+                nc.vector.tensor_scalar_mul(
+                    out=a_term[:, r, :].rearrange("p (i t j) -> p i t j", i=NL, t=T),
+                    in0=scale_sb[:, r, :].rearrange("p (i j t) -> p i t j", i=NL, t=T),
+                    scalar1=mask_h[:, r : r + 1],
+                )
+
+            def product(name, block):
+                acc = psum.tile([P, ROWS], F32, name="acc")
+                cols = slice(block * P, (block + 1) * P)
+                for r in range(ROW_TILES):
+                    for c in range(PASSES):
+                        nc.tensor.matmul_mx(
+                            out=acc[:, r * P : (r + 1) * P],
+                            lhsT=codes[name][:, c, cols].bitcast(FP8X4),
+                            lhsT_scale=scales[name][:, c, cols],
+                            rhs=x_codes[:, r, c, :].bitcast(FP8X4),
+                            rhs_scale=x_scales[:, r, c, :],
+                            start=(c == 0),
+                            stop=(c == PASSES - 1),
+                        )
+                return acc
+
+            e2_cols = load.tile([P, JKU * G // P, ROWS], F32, name="e2_cols")
+            for block in range(JKU * G // P):
+                acc = product("tpv", block)
+                nc.scalar.activation(
+                    out=e2_cols[:, block, :], in_=acc[:], func=FUNC.Exp, bias=v_bias2[:, block : block + 1], scale=2.0
+                )
+                nc.vector.tensor_scalar(
+                    out=e2_cols[:, block, :],
+                    in0=e2_cols[:, block, :],
+                    scalar1=math.exp(2.0),
+                    scalar2=math.exp(-2.0),
+                    op0=ALU.min,
+                    op1=ALU.max,
+                )
+            for r in range(ROW_TILES):
+                for h in range(2):
+                    back = psum.tile([P, 4 * P], F32, name="back")
+                    for q in range(4):
+                        nc.tensor.transpose(
+                            back[:, q * P : (q + 1) * P], e2_cols[:, 4 * h + q, r * P : (r + 1) * P], ident[:]
+                        )
+                    nc.vector.tensor_copy(
+                        out=e2[:, r, :, h * 2 * P : (h + 1) * 2 * P], in_=back[:].rearrange("p (a g) -> p g a", g=G)
+                    )
+
+            for block in range(JKU * G // P):
+                acc = product("tpm", block)
+                nc.scalar.activation(
+                    out=m2_cols[:, block, :], in_=acc[:], func=FUNC.Identity, bias=m_bias[:, block : block + 1], scale=1.0
+                )
+                nc.vector.tensor_scalar(
+                    out=m2_cols[:, block, :],
+                    in0=m2_cols[:, block, :],
+                    scalar1=1.0,
+                    scalar2=-1.0,
+                    op0=ALU.min,
+                    op1=ALU.max,
+                )
+
+            tw_cols = load.tile([P, JKU // P, ROWS], F32, name="tw_cols")
+            for block in range(JKU // P):
+                acc = product("tw", block)
+                nc.scalar.activation(
+                    out=tw_cols[:, block, :], in_=acc[:], func=FUNC.Identity, bias=tw_bias[:, block : block + 1], scale=1.0
+                )
+            for r in range(ROW_TILES):
+                back = psum.tile([P, 4 * P], F32, name="back")
+                for q in range(4):
+                    nc.tensor.transpose(back[:, q * P : (q + 1) * P], tw_cols[:, q, r * P : (r + 1) * P], ident[:])
+                nc.vector.tensor_scalar_mul(out=b_term[:, r, :], in0=back[:], scalar1=c_pos[:, r : r + 1])
+
+        resident = ctx.enter_context(tc.psum_pool(name="resident", bufs=1))
+        m2 = {}
+        for r in range(ROW_TILES):
+            for h in range(2):
+                m2[(r, h)] = resident.tile([P, 4 * P], F32, name="m2_%d_%d" % (r, h))
+                for q in range(4):
+                    nc.tensor.transpose(
+                        m2[(r, h)][:, q * P : (q + 1) * P], m2_cols[:, 4 * h + q, r * P : (r + 1) * P], ident[:]
+                    )
+
+        roots_pool = ctx.enter_context(tc.tile_pool(name="roots", bufs=3))
+        diff_pool = ctx.enter_context(tc.tile_pool(name="diff", bufs=3))
+        sum_pool = ctx.enter_context(tc.tile_pool(name="sum", bufs=4))
+        prod_pool = ctx.enter_context(tc.tile_pool(name="prod", bufs=LN_BLOCK + 2))
+        out_pool = ctx.enter_context(tc.tile_pool(name="outp", bufs=LN_BLOCK))
+        roots = {}
+        diffs = {}
+        sums = {}
+        prods = {}
+        outs = {}
+
+        def chunk_slots(n):
+            i = n % NL
+            return [
+                (g, j, ((i * NL + j) * T + t) * G + g, slice((t * NL + j) * KU, (t * NL + j + 1) * KU))
+                for g in range(G)
+                for t in range(T)
+                for j in range(NL)
+            ]
+
+        def make_roots(n):
+            r = n // NL
+            roots[n] = roots_pool.tile([P, G, GRID], F32, name="root")
+            for g, j, col, where in chunk_slots(n):
+                nc.scalar.activation(
+                    out=roots[n][:, g, where],
+                    in_=e2[:, r, g, j * KU : (j + 1) * KU],
+                    func=FUNC.Abs_reciprocal_sqrt,
+                    bias=e1[:, r, col : col + 1],
+                    scale=1.0,
+                )
+
+        def make_diffs(n):
+            r = n // NL
+            diffs[n] = diff_pool.tile([P, G, GRID], F32, name="diff")
+            for g, j, col, where in chunk_slots(n):
+                m2_view = m2[(r, j // 8)][:].rearrange("p (j a g) -> p j g a", j=8, g=G)
+                nc.vector.scalar_tensor_tensor(
+                    out=diffs[n][:, g, where],
+                    in0=m2_view[:, j % 8, g, :],
+                    scalar=m1[:, r, col : col + 1],
+                    in1=roots[n][:, g, where],
+                    op0=ALU.subtract,
+                    op1=ALU.mult,
+                )
+
+        def square_diffs(n):
+            nc.scalar.activation(out=diffs[n][:], in_=diffs[n][:], func=FUNC.Square, scale=math.sqrt(0.5))
+
+        def multiply_roots(n):
+            prods[n] = prod_pool.tile([P, GRID], F32, name="prod")
+            nc.vector.tensor_tensor(
+                out=prods[n][:].rearrange("p (a t u) -> p a t u", t=T, u=T),
+                in0=roots[n][:, 0, :].rearrange("p (t a u) -> p a t u", t=T, u=T),
+                in1=roots[n][:, 1, :].rearrange("p (t a u) -> p a t u", t=T, u=T),
+                op=ALU.mult,
+            )
+
+        def add_squares(n):
+            sums[n] = sum_pool.tile([P, GRID], F32, name="sum")
+            nc.vector.tensor_tensor(out=sums[n][:], in0=diffs[n][:, 0, :], in1=diffs[n][:, 1, :], op=ALU.add)
+
+        def add_child_term(n):
+            r, i = n // NL, n % NL
+            view = sums[n][:].rearrange("p (s v) -> p s v", v=KU)
+            nc.vector.scalar_tensor_tensor(
+                out=view,
+                in0=view,
+                scalar=c_neg[:, r : r + 1],
+                in1=a_term[:, r, i * T * NL : (i + 1) * T * NL].unsqueeze(2).to_broadcast([P, T * NL, KU]),
+                op0=ALU.mult,
+                op1=ALU.add,
+            )
+
+        def add_parent_term(n):
+            r = n // NL
+            outs[n] = out_pool.tile([P, GRID], F32, name="outt")
+            nc.vector.tensor_tensor(
+                out=outs[n][:].rearrange("p (a t u) -> p a t u", t=T, u=T),
+                in0=sums[n][:].rearrange("p (t a u) -> p a t u", t=T, u=T),
+                in1=b_term[:, r, :].rearrange("p (a u) -> p a u", u=T).unsqueeze(2).to_broadcast([P, NL * NL, T, T]),
+                op=ALU.add,
+            )
+
+        def take_log(n):
+            nc.scalar.activation(out=prods[n][:], in_=prods[n][:], func=FUNC.Ln)
+
+        def finish(n):
+            r, i = n // NL, n % NL
+            nc.vector.scalar_tensor_tensor(
+                out=outs[n][:],
+                in0=prods[n][:],
+                scalar=c_pos[:, r : r + 1],
+                in1=outs[n][:],
+                op0=ALU.mult,
+                op1=ALU.add,
+            )
+            nc.sync.dma_start(out=out_rows[r * P : (r + 1) * P, i, :], in_=outs[n][:])
+
+        def live(n):
+            return 0 <= n < CHUNKS
+
+        for step in range(CHUNKS + FINAL_LAG + 1):
+            if live(step):
+                make_roots(step)
+            if live(step - 1):
+                make_diffs(step - 1)
+                square_diffs(step - 1)
+                multiply_roots(step - 1)
+            if live(step - 2):
+                add_squares(step - 2)
+            if live(step - 3):
+                add_child_term(step - 3)
+            if live(step - 4):
+                add_parent_term(step - 4)
+            if live(step - 1) and step % LN_BLOCK == 0:
+                for n in range(step - LN_BLOCK, step):
+                    take_log(n)
+            if live(step - FINAL_LAG):
+                finish(step - FINAL_LAG)

@@ -307,7 +307,7 @@ def tile_chainlveg_pb_kernel(
 
         def multiply_roots(n):
             prods[n] = prod_pool.tile([P, GRID], F32, name="prod")
-            nc.vector.tensor_tensor(
+            nc.gpsimd.tensor_tensor(
                 out=prods[n][:].rearrange("p (a t u) -> p a t u", t=T, u=T),
                 in0=roots[n][:, 0, :].rearrange("p (t a u) -> p a t u", t=T, u=T),
                 in1=roots[n][:, 1, :].rearrange("p (t a u) -> p a t u", t=T, u=T),

@@ -26,11 +26,12 @@ KU = NL * T
 JKU = NL * KU
 CS = NL * NL * T * G
 GRID = NL * NL * T * T
+BANK = 512
 PIECE = 512
 LOG_2PI = math.log(2.0 * math.pi)
 CHUNKS = ROW_TILES * NL
 LN_BLOCK = 8
-FINAL_LAG = LN_BLOCK + 1
+FINAL_LAG = LN_BLOCK + 2
 
 FLOPS = 2 * ROWS * D * (JKU + 2 * JKU * G)
 
@@ -51,14 +52,15 @@ def tile_chainlveg_pb_kernel(
     with ExitStack() as ctx:
         ctx.enter_context(tc.manual_schedule())
         keep = ctx.enter_context(tc.tile_pool(name="keep", bufs=1))
+        work = ctx.enter_context(tc.psum_pool(name="work", bufs=2))
+        resident = ctx.enter_context(tc.psum_pool(name="resident", bufs=1))
 
         ident = keep.tile([P, P], F32, name="ident")
         e1 = keep.tile([P, ROW_TILES, CS], F32, name="e1")
         m1 = keep.tile([P, ROW_TILES, CS], F32, name="m1")
         e2 = keep.tile([P, ROW_TILES, G, JKU], F32, name="e2")
-        a_term = keep.tile([P, ROW_TILES, NL * T * NL], F32, name="a_term")
-        b_term = keep.tile([P, ROW_TILES, JKU], F32, name="b_term")
-        m2_cols = keep.tile([P, JKU * G // P, ROWS], F32, name="m2_cols")
+        a_cols = keep.tile([P, JKU // P, ROWS], F32, name="a_cols")
+        b_cols = keep.tile([P, JKU // P, ROWS], F32, name="b_cols")
         small = keep.tile([P, 32], F32, name="small")
         tw_bias = keep.tile([P, 4], F32, name="tw_bias")
         v_bias2 = keep.tile([P, 8], F32, name="v_bias2")
@@ -67,14 +69,20 @@ def tile_chainlveg_pb_kernel(
         m_bias = small[:, 4:12]
         mask_h = small[:, 20:23]
         mask_n = small[:, 23:26]
+        m2 = {}
 
         make_identity(nc, ident[:])
+
+        def to_rows(dst, cols, first_block, r):
+            for q in range(BANK // P):
+                nc.tensor.transpose(
+                    dst[:, q * P : (q + 1) * P], cols[:, first_block + q, r * P : (r + 1) * P], ident[:]
+                )
 
         with ExitStack() as pro:
             load = pro.enter_context(tc.tile_pool(name="load", bufs=1))
             group = pro.enter_context(tc.tile_pool(name="group", bufs=3))
             quant = pro.enter_context(tc.tile_pool(name="quant", bufs=1))
-            psum = pro.enter_context(tc.psum_pool(name="psum", bufs=2))
 
             rows_bf = load.tile([P, P], BF16, name="rows_bf")
             nc.vector.memset(rows_bf[:], 0.0)
@@ -111,8 +119,8 @@ def tile_chainlveg_pb_kernel(
 
             rows_f = load.tile([P, P], F32, name="rows_f")
             nc.vector.tensor_copy(out=rows_f[:], in_=rows_bf[:])
-            small_ps = psum.tile([P, P], F32, name="small_ps", bufs=1)
-            nc.tensor.transpose(small_ps[:], rows_f[:], ident[:])
+            small_ps = work.tile([P, BANK], F32, name="bank")
+            nc.tensor.transpose(small_ps[:, 0:P], rows_f[:], ident[:])
             nc.vector.tensor_copy(out=small[:], in_=small_ps[:, 0:32])
             nc.vector.tensor_scalar_add(out=tw_bias[:], in0=small[:, 0:4], scalar1=-LOG_2PI)
             nc.vector.tensor_scalar_mul(out=v_bias2[:], in0=small[:, 12:20], scalar1=2.0)
@@ -127,12 +135,12 @@ def tile_chainlveg_pb_kernel(
             )
             for r in range(ROW_TILES):
                 x_words = x_sb[:, r, :].bitcast(F32)
-                xt = psum.tile([P, PASSES, 2, P], F32, name="xt")
-                for c in range(PASSES):
-                    for u in range(2):
-                        first = (c * 2 + u) * P
-                        nc.tensor.transpose(xt[:, c, u, :], x_words[:, first : first + P], ident[:])
-                nc.vector.tensor_copy(out=x_group_words[:, r], in_=xt[:].rearrange("p c u m -> p c m u"))
+                xt = work.tile([P, BANK], F32, name="bank")
+                for cu in range(PASSES * 2):
+                    nc.tensor.transpose(xt[:, cu * P : (cu + 1) * P], x_words[:, cu * P : (cu + 1) * P], ident[:])
+                nc.vector.tensor_copy(
+                    out=x_group_words[:, r], in_=xt[:].rearrange("p (c u m) -> p c m u", c=PASSES, u=2)
+                )
             per_tile = PASSES * P * PACK
             for r in range(ROW_TILES):
                 nc.vector.quantize_mx(
@@ -146,41 +154,28 @@ def tile_chainlveg_pb_kernel(
             for name in ("tpv", "tpm", "tw"):
                 codes[name] = quant.tile([P, PASSES, widths[name]], U32, name="codes_" + name, align_bytes=64)
                 scales[name] = quant.tile([P, PASSES, widths[name]], U8, name="scales_" + name, align_bytes=64)
-            units = [(name, c) for name in ("tpv", "tpm", "tw") for c in range(PASSES)]
-            grouped = {}
-            pieces_done = 0
-            for index in range(len(units) + 1):
-                if index < len(units):
-                    name, c = units[index]
-                    grouped[index] = group.tile([P, PACK * JKU * G], BF16, name="grouped", align_bytes=64)
+
+            def quantise_weight(name, scalar_helps):
+                grouped = {}
+                for c in range(PASSES):
+                    grouped[c] = group.tile([P, PACK * JKU * G], BF16, name="grouped", align_bytes=64)
                     src = raw[name][:, c, :].rearrange("p (t a i) -> p a t i", t=PACK, i=4)
-                    dst = grouped[index][:, 0 : PACK * widths[name]].rearrange("p (a i t) -> p a t i", i=4, t=PACK)
+                    dst = grouped[c][:, 0 : PACK * widths[name]].rearrange("p (a i t) -> p a t i", i=4, t=PACK)
                     for h in range(widths[name] // PIECE):
                         runs = slice(h * PIECE // 4, (h + 1) * PIECE // 4)
-                        if pieces_done % 2 == 0:
-                            nc.vector.tensor_copy(out=dst[:, runs], in_=src[:, runs])
-                        else:
+                        if scalar_helps and h % 2 == 1:
                             nc.scalar.copy(out=dst[:, runs], in_=src[:, runs])
-                        pieces_done += 1
-                if index > 0:
-                    name, c = units[index - 1]
+                        else:
+                            nc.vector.tensor_copy(out=dst[:, runs], in_=src[:, runs])
+                for c in range(PASSES):
                     nc.vector.quantize_mx(
                         out=codes[name][:, c, :].bitcast(FP8X4),
                         scales=scales[name][:, c, :],
-                        in_=grouped[index - 1][:, 0 : PACK * widths[name]],
+                        in_=grouped[c][:, 0 : PACK * widths[name]],
                     )
 
-            for r in range(ROW_TILES):
-                nc.scalar.activation(out=e1[:, r, :], in_=var_sb[:, r, :], func=FUNC.Exp, scale=2.0)
-                nc.vector.tensor_copy(out=m1[:, r, :], in_=mu_sb[:, r, :])
-                nc.vector.tensor_scalar_mul(
-                    out=a_term[:, r, :].rearrange("p (i t j) -> p i t j", i=NL, t=T),
-                    in0=scale_sb[:, r, :].rearrange("p (i j t) -> p i t j", i=NL, t=T),
-                    scalar1=mask_h[:, r : r + 1],
-                )
-
             def product(name, block):
-                acc = psum.tile([P, ROWS], F32, name="acc")
+                acc = work.tile([P, BANK], F32, name="bank")
                 cols = slice(block * P, (block + 1) * P)
                 for r in range(ROW_TILES):
                     for c in range(PASSES):
@@ -195,77 +190,104 @@ def tile_chainlveg_pb_kernel(
                         )
                 return acc
 
+            quantise_weight("tpv", True)
+            for r in range(ROW_TILES):
+                nc.scalar.activation(out=e1[:, r, :], in_=var_sb[:, r, :], func=FUNC.Exp, scale=2.0)
+            quantise_weight("tpm", False)
+
             e2_cols = load.tile([P, JKU * G // P, ROWS], F32, name="e2_cols")
             for block in range(JKU * G // P):
                 acc = product("tpv", block)
                 nc.scalar.activation(
-                    out=e2_cols[:, block, :], in_=acc[:], func=FUNC.Exp, bias=v_bias2[:, block : block + 1], scale=2.0
-                )
-                nc.vector.tensor_scalar(
                     out=e2_cols[:, block, :],
-                    in0=e2_cols[:, block, :],
-                    scalar1=math.exp(2.0),
-                    scalar2=math.exp(-2.0),
-                    op0=ALU.min,
-                    op1=ALU.max,
+                    in_=acc[:, 0:ROWS],
+                    func=FUNC.Exp,
+                    bias=v_bias2[:, block : block + 1],
+                    scale=2.0,
                 )
             for r in range(ROW_TILES):
                 for h in range(2):
-                    back = psum.tile([P, 4 * P], F32, name="back")
-                    for q in range(4):
-                        nc.tensor.transpose(
-                            back[:, q * P : (q + 1) * P], e2_cols[:, 4 * h + q, r * P : (r + 1) * P], ident[:]
-                        )
-                    nc.vector.tensor_copy(
-                        out=e2[:, r, :, h * 2 * P : (h + 1) * 2 * P], in_=back[:].rearrange("p (a g) -> p g a", g=G)
+                    back = work.tile([P, BANK], F32, name="bank")
+                    to_rows(back, e2_cols, 4 * h, r)
+                    nc.vector.tensor_scalar(
+                        out=e2[:, r, :, h * BANK // G : (h + 1) * BANK // G],
+                        in0=back[:].rearrange("p (a g) -> p g a", g=G),
+                        scalar1=math.exp(2.0),
+                        scalar2=math.exp(-2.0),
+                        op0=ALU.min,
+                        op1=ALU.max,
                     )
+            for r in range(ROW_TILES):
+                nc.vector.tensor_copy(out=m1[:, r, :], in_=mu_sb[:, r, :])
 
+            m2_cols = load.tile([P, JKU * G // P, ROWS], F32, name="m2_cols")
             for block in range(JKU * G // P):
                 acc = product("tpm", block)
-                nc.scalar.activation(
-                    out=m2_cols[:, block, :], in_=acc[:], func=FUNC.Identity, bias=m_bias[:, block : block + 1], scale=1.0
-                )
                 nc.vector.tensor_scalar(
                     out=m2_cols[:, block, :],
-                    in0=m2_cols[:, block, :],
-                    scalar1=1.0,
-                    scalar2=-1.0,
-                    op0=ALU.min,
-                    op1=ALU.max,
+                    in0=acc[:, 0:ROWS],
+                    scalar1=m_bias[:, block : block + 1],
+                    scalar2=1.0,
+                    op0=ALU.add,
+                    op1=ALU.min,
                 )
+            nc.vector.tensor_scalar_max(out=m2_cols[:], in0=m2_cols[:], scalar1=-1.0)
+            for r in range(ROW_TILES):
+                for h in range(2):
+                    m2[(r, h)] = resident.tile([P, BANK], F32, name="m2_%d_%d" % (r, h))
+                    to_rows(m2[(r, h)], m2_cols, 4 * h, r)
 
-            tw_cols = load.tile([P, JKU // P, ROWS], F32, name="tw_cols")
+            quantise_weight("tw", False)
+            c_bank = work.tile([P, BANK], F32, name="bank")
+            for r in range(ROW_TILES):
+                nc.tensor.transpose(c_bank[:, r * P : (r + 1) * P], c_pos[:, r : r + 1].to_broadcast([P, P]), ident[:])
+            c_rows = load.tile([P, ROWS], F32, name="c_rows")
+            nc.vector.tensor_copy(out=c_rows[:], in_=c_bank[:, 0:ROWS])
             for block in range(JKU // P):
                 acc = product("tw", block)
-                nc.scalar.activation(
-                    out=tw_cols[:, block, :], in_=acc[:], func=FUNC.Identity, bias=tw_bias[:, block : block + 1], scale=1.0
+                nc.vector.scalar_tensor_tensor(
+                    out=b_cols[:, block, :],
+                    in0=acc[:, 0:ROWS],
+                    scalar=tw_bias[:, block : block + 1],
+                    in1=c_rows[:],
+                    op0=ALU.add,
+                    op1=ALU.mult,
                 )
+
+            a_rows = load.tile([P, ROW_TILES, JKU], F32, name="a_rows")
             for r in range(ROW_TILES):
-                back = psum.tile([P, 4 * P], F32, name="back")
-                for q in range(4):
-                    nc.tensor.transpose(back[:, q * P : (q + 1) * P], tw_cols[:, q, r * P : (r + 1) * P], ident[:])
-                nc.vector.tensor_scalar_mul(out=b_term[:, r, :], in0=back[:], scalar1=c_pos[:, r : r + 1])
+                nc.vector.tensor_scalar_mul(
+                    out=a_rows[:, r, :].rearrange("p (i t j) -> p i t j", i=NL, t=T),
+                    in0=scale_sb[:, r, :].rearrange("p (i j t) -> p i t j", i=NL, t=T),
+                    scalar1=mask_h[:, r : r + 1],
+                )
+                turned = work.tile([P, BANK], F32, name="bank")
+                for q in range(BANK // P):
+                    nc.tensor.transpose(turned[:, q * P : (q + 1) * P], a_rows[:, r, q * P : (q + 1) * P], ident[:])
+                nc.vector.tensor_copy(
+                    out=a_cols[:, :, r * P : (r + 1) * P], in_=turned[:].rearrange("p (q m) -> p q m", m=P)
+                )
 
-        resident = ctx.enter_context(tc.psum_pool(name="resident", bufs=1))
-        m2 = {}
-        for r in range(ROW_TILES):
-            for h in range(2):
-                m2[(r, h)] = resident.tile([P, 4 * P], F32, name="m2_%d_%d" % (r, h))
-                for q in range(4):
-                    nc.tensor.transpose(
-                        m2[(r, h)][:, q * P : (q + 1) * P], m2_cols[:, 4 * h + q, r * P : (r + 1) * P], ident[:]
-                    )
-
-        roots_pool = ctx.enter_context(tc.tile_pool(name="roots", bufs=3))
-        diff_pool = ctx.enter_context(tc.tile_pool(name="diff", bufs=3))
-        sum_pool = ctx.enter_context(tc.tile_pool(name="sum", bufs=4))
-        prod_pool = ctx.enter_context(tc.tile_pool(name="prod", bufs=LN_BLOCK + 2))
-        out_pool = ctx.enter_context(tc.tile_pool(name="outp", bufs=LN_BLOCK))
+        roots_pool = ctx.enter_context(tc.tile_pool(name="roots", bufs=3, reuse_waits="tile"))
+        diff_pool = ctx.enter_context(tc.tile_pool(name="diff", bufs=4, reuse_waits="tile"))
+        sum_pool = ctx.enter_context(tc.tile_pool(name="sum", bufs=4, reuse_waits="tile"))
+        prod_pool = ctx.enter_context(tc.tile_pool(name="prod", bufs=LN_BLOCK + 3, reuse_waits="tile"))
+        out_pool = ctx.enter_context(tc.tile_pool(name="outp", bufs=LN_BLOCK, reuse_waits="tile"))
         roots = {}
         diffs = {}
         sums = {}
         prods = {}
         outs = {}
+        a_term = {}
+        b_term = {}
+
+        def place_child_term(r):
+            a_term[r] = work.tile([P, BANK], F32, name="bank")
+            to_rows(a_term[r], a_cols, 0, r)
+
+        def place_parent_term(r):
+            b_term[r] = work.tile([P, BANK], F32, name="bank")
+            to_rows(b_term[r], b_cols, 0, r)
 
         def chunk_slots(n):
             i = n % NL
@@ -316,7 +338,7 @@ def tile_chainlveg_pb_kernel(
 
         def add_squares(n):
             sums[n] = sum_pool.tile([P, GRID], F32, name="sum")
-            nc.vector.tensor_tensor(out=sums[n][:], in0=diffs[n][:, 0, :], in1=diffs[n][:, 1, :], op=ALU.add)
+            nc.gpsimd.tensor_tensor(out=sums[n][:], in0=diffs[n][:, 0, :], in1=diffs[n][:, 1, :], op=ALU.add)
 
         def add_child_term(n):
             r, i = n // NL, n % NL
@@ -325,20 +347,24 @@ def tile_chainlveg_pb_kernel(
                 out=view,
                 in0=view,
                 scalar=c_neg[:, r : r + 1],
-                in1=a_term[:, r, i * T * NL : (i + 1) * T * NL].unsqueeze(2).to_broadcast([P, T * NL, KU]),
+                in1=a_term[r][:, i * T * NL : (i + 1) * T * NL].unsqueeze(2).to_broadcast([P, T * NL, KU]),
                 op0=ALU.mult,
                 op1=ALU.add,
             )
+            if i == NL - 1 and r + 1 < ROW_TILES:
+                place_child_term(r + 1)
 
         def add_parent_term(n):
-            r = n // NL
+            r, i = n // NL, n % NL
             outs[n] = out_pool.tile([P, GRID], F32, name="outt")
             nc.vector.tensor_tensor(
                 out=outs[n][:].rearrange("p (a t u) -> p a t u", t=T, u=T),
                 in0=sums[n][:].rearrange("p (t a u) -> p a t u", t=T, u=T),
-                in1=b_term[:, r, :].rearrange("p (a u) -> p a u", u=T).unsqueeze(2).to_broadcast([P, NL * NL, T, T]),
+                in1=b_term[r][:].rearrange("p (a u) -> p a u", u=T).unsqueeze(2).to_broadcast([P, NL * NL, T, T]),
                 op=ALU.add,
             )
+            if i == NL - 1 and r + 1 < ROW_TILES:
+                place_parent_term(r + 1)
 
         def take_log(n):
             nc.scalar.activation(out=prods[n][:], in_=prods[n][:], func=FUNC.Ln)
@@ -358,21 +384,24 @@ def tile_chainlveg_pb_kernel(
         def live(n):
             return 0 <= n < CHUNKS
 
+        place_child_term(0)
+        place_parent_term(0)
         for step in range(CHUNKS + FINAL_LAG + 1):
             if live(step):
                 make_roots(step)
             if live(step - 1):
                 make_diffs(step - 1)
-                square_diffs(step - 1)
                 multiply_roots(step - 1)
             if live(step - 2):
-                add_squares(step - 2)
+                square_diffs(step - 2)
             if live(step - 3):
-                add_child_term(step - 3)
+                add_squares(step - 3)
             if live(step - 4):
-                add_parent_term(step - 4)
-            if live(step - 1) and step % LN_BLOCK == 0:
-                for n in range(step - LN_BLOCK, step):
+                add_child_term(step - 4)
+            if live(step - 5):
+                add_parent_term(step - 5)
+            if live(step - 2) and (step - 1) % LN_BLOCK == 0:
+                for n in range(step - 1 - LN_BLOCK, step - 1):
                     take_log(n)
             if live(step - FINAL_LAG):
                 finish(step - FINAL_LAG)

@@ -30,8 +30,9 @@ BANK = 512
 PIECE = 512
 LOG_2PI = math.log(2.0 * math.pi)
 CHUNKS = ROW_TILES * NL
-LN_BLOCK = 8
+LN_BLOCK = 12
 FINAL_LAG = LN_BLOCK + 2
+ROOT_LEAD = 3
 
 FLOPS = 2 * ROWS * D * (JKU + 2 * JKU * G)
 
@@ -57,7 +58,7 @@ def tile_chainlveg_pb_kernel(
 
         ident = keep.tile([P, P], F32, name="ident")
         e1 = keep.tile([P, ROW_TILES, CS], F32, name="e1")
-        m1 = keep.tile([P, ROW_TILES, CS], F32, name="m1")
+        m1 = keep.tile([P, ROW_TILES, CS], BF16, name="m1")
         e2 = keep.tile([P, ROW_TILES, G, JKU], F32, name="e2")
         a_cols = keep.tile([P, JKU // P, ROWS], F32, name="a_cols")
         b_cols = keep.tile([P, JKU // P, ROWS], F32, name="b_cols")
@@ -85,6 +86,18 @@ def tile_chainlveg_pb_kernel(
             quant = pro.enter_context(tc.tile_pool(name="quant", bufs=1))
 
             rows_bf = load.tile([P, P], BF16, name="rows_bf")
+            rows_f = load.tile([P, P], F32, name="rows_f")
+            x_sb = load.tile([P, ROW_TILES, D], BF16, name="x_sb")
+            raw = {}
+            raw["tpv"] = load.tile([P, PASSES, PACK * widths["tpv"]], BF16, name="raw_tpv")
+            var_sb = load.tile([P, ROW_TILES, CS], BF16, name="var_sb")
+            raw["tpm"] = load.tile([P, PASSES, PACK * widths["tpm"]], BF16, name="raw_tpm")
+            e2_cols = load.tile([P, JKU * G // P, ROWS], F32, name="e2_cols")
+            m2_cols = load.tile([P, JKU * G // P, ROWS], F32, name="m2_cols")
+            raw["tw"] = load.tile([P, PASSES, PACK * widths["tw"]], BF16, name="raw_tw")
+            scale_sb = load.tile([P, ROW_TILES, CS // G], BF16, name="scale_sb")
+            c_rows = load.tile([P, ROWS], F32, name="c_rows")
+            a_rows = load.tile([P, ROW_TILES, JKU], F32, name="a_rows")
             nc.vector.memset(rows_bf[:], 0.0)
             nc.scalar.dma_start(out=rows_bf[0:4, :], in_=tw_b.rearrange("(r p) -> r p", p=P))
             nc.scalar.dma_start(out=rows_bf[4:12, :], in_=tpm_b.rearrange("(r p) -> r p", p=P))
@@ -96,14 +109,7 @@ def tile_chainlveg_pb_kernel(
                 out=rows_bf[23:26, :], in_=mask_next.rearrange("b q -> (b q)").rearrange("(r p) -> r p", p=P)
             )
 
-            x_sb = load.tile([P, ROW_TILES, D], BF16, name="x_sb")
             nc.sync.dma_start(out=x_sb[:], in_=x_rows)
-            raw = {}
-            for name in ("tpv", "tpm", "tw"):
-                raw[name] = load.tile([P, PASSES, PACK * widths[name]], BF16, name="raw_" + name)
-            var_sb = load.tile([P, ROW_TILES, CS], BF16, name="var_sb")
-            mu_sb = load.tile([P, ROW_TILES, CS], BF16, name="mu_sb")
-            scale_sb = load.tile([P, ROW_TILES, CS // G], BF16, name="scale_sb")
 
             def load_weight(name):
                 view = weights[name].rearrange("(c u p e) n -> c p u (e n)", c=PASSES, u=2, p=P, e=2)
@@ -113,19 +119,9 @@ def tile_chainlveg_pb_kernel(
             load_weight("tpv")
             nc.sync.dma_start(out=var_sb[:], in_=var_rows)
             load_weight("tpm")
-            nc.sync.dma_start(out=mu_sb[:], in_=mu_rows)
+            nc.sync.dma_start(out=m1[:], in_=mu_rows)
             load_weight("tw")
             nc.sync.dma_start(out=scale_sb[:], in_=scale_rows)
-
-            rows_f = load.tile([P, P], F32, name="rows_f")
-            nc.vector.tensor_copy(out=rows_f[:], in_=rows_bf[:])
-            small_ps = work.tile([P, BANK], F32, name="bank")
-            nc.tensor.transpose(small_ps[:, 0:P], rows_f[:], ident[:])
-            nc.vector.tensor_copy(out=small[:], in_=small_ps[:, 0:32])
-            nc.vector.tensor_scalar_add(out=tw_bias[:], in0=small[:, 0:4], scalar1=-LOG_2PI)
-            nc.vector.tensor_scalar_mul(out=v_bias2[:], in0=small[:, 12:20], scalar1=2.0)
-            nc.vector.tensor_tensor(out=c_pos[:], in0=mask_h, in1=mask_n, op=ALU.mult)
-            nc.vector.tensor_scalar_mul(out=c_neg[:], in0=c_pos[:], scalar1=-1.0)
 
             x_group = quant.tile([P, ROW_TILES * PASSES * P * PACK], BF16, name="x_group", align_bytes=64)
             x_codes = quant.tile([P, ROW_TILES, PASSES, P], U32, name="x_codes", align_bytes=64)
@@ -141,6 +137,15 @@ def tile_chainlveg_pb_kernel(
                 nc.vector.tensor_copy(
                     out=x_group_words[:, r], in_=xt[:].rearrange("p (c u m) -> p c m u", c=PASSES, u=2)
                 )
+            nc.vector.tensor_copy(out=rows_f[:], in_=rows_bf[:])
+            small_ps = work.tile([P, BANK], F32, name="bank")
+            nc.tensor.transpose(small_ps[:, 0:P], rows_f[:], ident[:])
+            nc.vector.tensor_copy(out=small[:], in_=small_ps[:, 0:32])
+            nc.vector.tensor_scalar_add(out=tw_bias[:], in0=small[:, 0:4], scalar1=-LOG_2PI)
+            nc.vector.tensor_scalar_mul(out=v_bias2[:], in0=small[:, 12:20], scalar1=2.0)
+            nc.vector.tensor_tensor(out=c_pos[:], in0=mask_h, in1=mask_n, op=ALU.mult)
+            nc.vector.tensor_scalar_mul(out=c_neg[:], in0=c_pos[:], scalar1=-1.0)
+
             per_tile = PASSES * P * PACK
             for r in range(ROW_TILES):
                 nc.vector.quantize_mx(
@@ -195,7 +200,6 @@ def tile_chainlveg_pb_kernel(
                 nc.scalar.activation(out=e1[:, r, :], in_=var_sb[:, r, :], func=FUNC.Exp, scale=2.0)
             quantise_weight("tpm", False)
 
-            e2_cols = load.tile([P, JKU * G // P, ROWS], F32, name="e2_cols")
             for block in range(JKU * G // P):
                 acc = product("tpv", block)
                 nc.scalar.activation(
@@ -217,10 +221,7 @@ def tile_chainlveg_pb_kernel(
                         op0=ALU.min,
                         op1=ALU.max,
                     )
-            for r in range(ROW_TILES):
-                nc.vector.tensor_copy(out=m1[:, r, :], in_=mu_sb[:, r, :])
 
-            m2_cols = load.tile([P, JKU * G // P, ROWS], F32, name="m2_cols")
             for block in range(JKU * G // P):
                 acc = product("tpm", block)
                 nc.vector.tensor_scalar(
@@ -241,7 +242,6 @@ def tile_chainlveg_pb_kernel(
             c_bank = work.tile([P, BANK], F32, name="bank")
             for r in range(ROW_TILES):
                 nc.tensor.transpose(c_bank[:, r * P : (r + 1) * P], c_pos[:, r : r + 1].to_broadcast([P, P]), ident[:])
-            c_rows = load.tile([P, ROWS], F32, name="c_rows")
             nc.vector.tensor_copy(out=c_rows[:], in_=c_bank[:, 0:ROWS])
             for block in range(JKU // P):
                 acc = product("tw", block)
@@ -254,7 +254,6 @@ def tile_chainlveg_pb_kernel(
                     op1=ALU.mult,
                 )
 
-            a_rows = load.tile([P, ROW_TILES, JKU], F32, name="a_rows")
             for r in range(ROW_TILES):
                 nc.vector.tensor_scalar_mul(
                     out=a_rows[:, r, :].rearrange("p (i t j) -> p i t j", i=NL, t=T),
@@ -268,11 +267,11 @@ def tile_chainlveg_pb_kernel(
                     out=a_cols[:, :, r * P : (r + 1) * P], in_=turned[:].rearrange("p (q m) -> p q m", m=P)
                 )
 
-        roots_pool = ctx.enter_context(tc.tile_pool(name="roots", bufs=3, reuse_waits="tile"))
-        diff_pool = ctx.enter_context(tc.tile_pool(name="diff", bufs=4, reuse_waits="tile"))
-        sum_pool = ctx.enter_context(tc.tile_pool(name="sum", bufs=4, reuse_waits="tile"))
+        roots_pool = ctx.enter_context(tc.tile_pool(name="roots", bufs=ROOT_LEAD + 3, reuse_waits="tile"))
+        diff_pool = ctx.enter_context(tc.tile_pool(name="diff", bufs=3, reuse_waits="tile"))
+        sum_pool = ctx.enter_context(tc.tile_pool(name="sum", bufs=3, reuse_waits="tile"))
         prod_pool = ctx.enter_context(tc.tile_pool(name="prod", bufs=LN_BLOCK + 3, reuse_waits="tile"))
-        out_pool = ctx.enter_context(tc.tile_pool(name="outp", bufs=LN_BLOCK, reuse_waits="tile"))
+        out_pool = ctx.enter_context(tc.tile_pool(name="outp", bufs=LN_BLOCK - 1, reuse_waits="tile"))
         roots = {}
         diffs = {}
         sums = {}
@@ -386,9 +385,11 @@ def tile_chainlveg_pb_kernel(
 
         place_child_term(0)
         place_parent_term(0)
+        for n in range(ROOT_LEAD):
+            make_roots(n)
         for step in range(CHUNKS + FINAL_LAG + 1):
-            if live(step):
-                make_roots(step)
+            if live(step + ROOT_LEAD):
+                make_roots(step + ROOT_LEAD)
             if live(step - 1):
                 make_diffs(step - 1)
                 multiply_roots(step - 1)

@@ -30,9 +30,12 @@ BANK = 512
 PIECE = 512
 LOG_2PI = math.log(2.0 * math.pi)
 CHUNKS = ROW_TILES * NL
-LN_BLOCK = 12
-FINAL_LAG = LN_BLOCK + 2
-ROOT_LEAD = 3
+HALVES = 2
+UNITS = CHUNKS * HALVES
+NJ = NL // HALVES
+HALF = GRID // HALVES
+BATCH = 12
+LEAD = BATCH + 6
 
 FLOPS = 2 * ROWS * D * (JKU + 2 * JKU * G)
 
@@ -53,20 +56,22 @@ def tile_chainlveg_pb_kernel(
     with ExitStack() as ctx:
         ctx.enter_context(tc.manual_schedule())
         keep = ctx.enter_context(tc.tile_pool(name="keep", bufs=1))
-        work = ctx.enter_context(tc.psum_pool(name="work", bufs=2))
+        work = ctx.enter_context(tc.psum_pool(name="work", bufs=4))
+        summed = ctx.enter_context(tc.psum_pool(name="summed", bufs=2))
         resident = ctx.enter_context(tc.psum_pool(name="resident", bufs=1))
 
         ident = keep.tile([P, P], F32, name="ident")
         e1 = keep.tile([P, ROW_TILES, CS], F32, name="e1")
         m1 = keep.tile([P, ROW_TILES, CS], BF16, name="m1")
         e2 = keep.tile([P, ROW_TILES, G, JKU], F32, name="e2")
-        a_cols = keep.tile([P, JKU // P, ROWS], F32, name="a_cols")
+        a_rows = keep.tile([P, ROW_TILES, JKU * T], F32, name="a_rows")
         b_cols = keep.tile([P, JKU // P, ROWS], F32, name="b_cols")
+        ch_rows = keep.tile([P, ROWS], F32, name="ch_rows")
+        m2_cols = keep.tile([P, JKU * G // P, ROWS], F32, name="m2_cols")
         small = keep.tile([P, 32], F32, name="small")
         tw_bias = keep.tile([P, 4], F32, name="tw_bias")
         v_bias2 = keep.tile([P, 8], F32, name="v_bias2")
         c_pos = keep.tile([P, ROW_TILES], F32, name="c_pos")
-        c_neg = keep.tile([P, ROW_TILES], F32, name="c_neg")
         m_bias = small[:, 4:12]
         mask_h = small[:, 20:23]
         mask_n = small[:, 23:26]
@@ -79,6 +84,11 @@ def tile_chainlveg_pb_kernel(
                 nc.tensor.transpose(
                     dst[:, q * P : (q + 1) * P], cols[:, first_block + q, r * P : (r + 1) * P], ident[:]
                 )
+
+        def place_m2(r):
+            for h in range(2):
+                m2[h] = resident.tile([P, BANK], F32, name="m2_%d" % h)
+                to_rows(m2[h], m2_cols, 4 * h, r)
 
         with ExitStack() as pro:
             load = pro.enter_context(tc.tile_pool(name="load", bufs=1))
@@ -93,11 +103,9 @@ def tile_chainlveg_pb_kernel(
             var_sb = load.tile([P, ROW_TILES, CS], BF16, name="var_sb")
             raw["tpm"] = load.tile([P, PASSES, PACK * widths["tpm"]], BF16, name="raw_tpm")
             e2_cols = load.tile([P, JKU * G // P, ROWS], F32, name="e2_cols")
-            m2_cols = load.tile([P, JKU * G // P, ROWS], F32, name="m2_cols")
             raw["tw"] = load.tile([P, PASSES, PACK * widths["tw"]], BF16, name="raw_tw")
             scale_sb = load.tile([P, ROW_TILES, CS // G], BF16, name="scale_sb")
             c_rows = load.tile([P, ROWS], F32, name="c_rows")
-            a_rows = load.tile([P, ROW_TILES, JKU], F32, name="a_rows")
             nc.vector.memset(rows_bf[:], 0.0)
             nc.scalar.dma_start(out=rows_bf[0:4, :], in_=tw_b.rearrange("(r p) -> r p", p=P))
             nc.scalar.dma_start(out=rows_bf[4:12, :], in_=tpm_b.rearrange("(r p) -> r p", p=P))
@@ -144,7 +152,6 @@ def tile_chainlveg_pb_kernel(
             nc.vector.tensor_scalar_add(out=tw_bias[:], in0=small[:, 0:4], scalar1=-LOG_2PI)
             nc.vector.tensor_scalar_mul(out=v_bias2[:], in0=small[:, 12:20], scalar1=2.0)
             nc.vector.tensor_tensor(out=c_pos[:], in0=mask_h, in1=mask_n, op=ALU.mult)
-            nc.vector.tensor_scalar_mul(out=c_neg[:], in0=c_pos[:], scalar1=-1.0)
 
             per_tile = PASSES * P * PACK
             for r in range(ROW_TILES):
@@ -233,16 +240,14 @@ def tile_chainlveg_pb_kernel(
                     op1=ALU.min,
                 )
             nc.vector.tensor_scalar_max(out=m2_cols[:], in0=m2_cols[:], scalar1=-1.0)
-            for r in range(ROW_TILES):
-                for h in range(2):
-                    m2[(r, h)] = resident.tile([P, BANK], F32, name="m2_%d_%d" % (r, h))
-                    to_rows(m2[(r, h)], m2_cols, 4 * h, r)
+            place_m2(0)
 
             quantise_weight("tw", False)
             c_bank = work.tile([P, BANK], F32, name="bank")
             for r in range(ROW_TILES):
                 nc.tensor.transpose(c_bank[:, r * P : (r + 1) * P], c_pos[:, r : r + 1].to_broadcast([P, P]), ident[:])
             nc.vector.tensor_copy(out=c_rows[:], in_=c_bank[:, 0:ROWS])
+            nc.vector.tensor_scalar_mul(out=ch_rows[:], in0=c_bank[:, 0:ROWS], scalar1=-0.5)
             for block in range(JKU // P):
                 acc = product("tw", block)
                 nc.vector.scalar_tensor_tensor(
@@ -256,153 +261,153 @@ def tile_chainlveg_pb_kernel(
 
             for r in range(ROW_TILES):
                 nc.vector.tensor_scalar_mul(
-                    out=a_rows[:, r, :].rearrange("p (i t j) -> p i t j", i=NL, t=T),
-                    in0=scale_sb[:, r, :].rearrange("p (i j t) -> p i t j", i=NL, t=T),
+                    out=a_rows[:, r, :].rearrange("p (s u) -> p s u", u=T),
+                    in0=scale_sb[:, r, :].unsqueeze(2).to_broadcast([P, JKU, T]),
                     scalar1=mask_h[:, r : r + 1],
                 )
-                turned = work.tile([P, BANK], F32, name="bank")
-                for q in range(BANK // P):
-                    nc.tensor.transpose(turned[:, q * P : (q + 1) * P], a_rows[:, r, q * P : (q + 1) * P], ident[:])
-                nc.vector.tensor_copy(
-                    out=a_cols[:, :, r * P : (r + 1) * P], in_=turned[:].rearrange("p (q m) -> p q m", m=P)
-                )
 
-        roots_pool = ctx.enter_context(tc.tile_pool(name="roots", bufs=ROOT_LEAD + 3, reuse_waits="tile"))
-        diff_pool = ctx.enter_context(tc.tile_pool(name="diff", bufs=3, reuse_waits="tile"))
-        sum_pool = ctx.enter_context(tc.tile_pool(name="sum", bufs=3, reuse_waits="tile"))
-        prod_pool = ctx.enter_context(tc.tile_pool(name="prod", bufs=LN_BLOCK + 3, reuse_waits="tile"))
-        out_pool = ctx.enter_context(tc.tile_pool(name="outp", bufs=LN_BLOCK - 1, reuse_waits="tile"))
+        logs_pool = ctx.enter_context(tc.tile_pool(name="logs", bufs=BATCH + 7, reuse_waits="tile"))
+        roots_pool = ctx.enter_context(tc.tile_pool(name="roots", bufs=BATCH, reuse_waits="tile"))
+        diff_pool = ctx.enter_context(tc.tile_pool(name="diff", bufs=4, reuse_waits="tile"))
+        turn_pool = ctx.enter_context(tc.tile_pool(name="turn", bufs=3, reuse_waits="tile"))
+        out_pool = ctx.enter_context(tc.tile_pool(name="outp", bufs=4, reuse_waits="tile"))
+        logs = {}
         roots = {}
         diffs = {}
+        gathered = {}
+        turned = {}
         sums = {}
-        prods = {}
         outs = {}
-        a_term = {}
-        b_term = {}
 
-        def place_child_term(r):
-            a_term[r] = work.tile([P, BANK], F32, name="bank")
-            to_rows(a_term[r], a_cols, 0, r)
-
-        def place_parent_term(r):
-            b_term[r] = work.tile([P, BANK], F32, name="bank")
-            to_rows(b_term[r], b_cols, 0, r)
-
-        def chunk_slots(n):
-            i = n % NL
+        def unit_slots(s):
+            i, h = (s // HALVES) % NL, s % HALVES
             return [
-                (g, j, ((i * NL + j) * T + t) * G + g, slice((t * NL + j) * KU, (t * NL + j + 1) * KU))
+                (g, j, ((i * NL + j) * T + t) * G + g, slice((t * NJ + j % NJ) * KU, (t * NJ + j % NJ + 1) * KU))
                 for g in range(G)
                 for t in range(T)
-                for j in range(NL)
+                for j in range(h * NJ, (h + 1) * NJ)
             ]
 
-        def make_roots(n):
-            r = n // NL
-            roots[n] = roots_pool.tile([P, G, GRID], F32, name="root")
-            for g, j, col, where in chunk_slots(n):
+        def take_logs(s):
+            r = s // (HALVES * NL)
+            logs[s] = logs_pool.tile([P, G, HALF], F32, name="log")
+            for g, j, col, where in unit_slots(s):
                 nc.scalar.activation(
-                    out=roots[n][:, g, where],
+                    out=logs[s][:, g, where],
                     in_=e2[:, r, g, j * KU : (j + 1) * KU],
-                    func=FUNC.Abs_reciprocal_sqrt,
+                    func=FUNC.Ln,
                     bias=e1[:, r, col : col + 1],
                     scale=1.0,
                 )
 
-        def make_diffs(n):
-            r = n // NL
-            diffs[n] = diff_pool.tile([P, G, GRID], F32, name="diff")
-            for g, j, col, where in chunk_slots(n):
-                m2_view = m2[(r, j // 8)][:].rearrange("p (j a g) -> p j g a", j=8, g=G)
+        def make_roots(s):
+            roots[s] = roots_pool.tile([P, G, HALF], F32, name="root")
+            nc.scalar.activation(out=roots[s][:], in_=logs[s][:], func=FUNC.Exp, scale=-0.5)
+
+        def make_diffs(s):
+            r = s // (HALVES * NL)
+            diffs[s] = diff_pool.tile([P, G, HALF], F32, name="diff")
+            for g, j, col, where in unit_slots(s):
+                m2_view = m2[j // 8][:].rearrange("p (j a g) -> p j g a", j=8, g=G)
                 nc.vector.scalar_tensor_tensor(
-                    out=diffs[n][:, g, where],
+                    out=diffs[s][:, g, where],
                     in0=m2_view[:, j % 8, g, :],
                     scalar=m1[:, r, col : col + 1],
-                    in1=roots[n][:, g, where],
+                    in1=roots[s][:, g, where],
                     op0=ALU.subtract,
                     op1=ALU.mult,
                 )
 
-        def square_diffs(n):
-            nc.scalar.activation(out=diffs[n][:], in_=diffs[n][:], func=FUNC.Square, scale=math.sqrt(0.5))
+        def square_diffs(s):
+            nc.gpsimd.tensor_tensor(out=diffs[s][:], in0=diffs[s][:], in1=diffs[s][:], op=ALU.mult)
 
-        def multiply_roots(n):
-            prods[n] = prod_pool.tile([P, GRID], F32, name="prod")
-            nc.gpsimd.tensor_tensor(
-                out=prods[n][:].rearrange("p (a t u) -> p a t u", t=T, u=T),
-                in0=roots[n][:, 0, :].rearrange("p (t a u) -> p a t u", t=T, u=T),
-                in1=roots[n][:, 1, :].rearrange("p (t a u) -> p a t u", t=T, u=T),
+        def gather(s):
+            gathered[s] = work.tile([P, BANK], F32, name="bank")
+            for q in range(BANK // P):
+                cols = slice(q * P, (q + 1) * P)
+                parts = [logs[s][:, 0, cols], logs[s][:, 1, cols], diffs[s][:, 0, cols], diffs[s][:, 1, cols]]
+                for w, part in enumerate(parts):
+                    nc.tensor.matmul(
+                        out=gathered[s][:, cols],
+                        lhsT=part,
+                        rhs=ident[:],
+                        is_transpose=True,
+                        start=(w == 0),
+                        stop=(w == len(parts) - 1),
+                    )
+
+        def scale_sum(s):
+            r = s // (HALVES * NL)
+            turned[s] = turn_pool.tile([P, HALF], F32, name="turned")
+            nc.vector.tensor_tensor(
+                out=turned[s][:].rearrange("p (q m) -> p q m", m=P),
+                in0=ch_rows[:, r * P : (r + 1) * P].unsqueeze(1).to_broadcast([P, BANK // P, P]),
+                in1=gathered[s][:].rearrange("p (q m) -> p q m", m=P),
                 op=ALU.mult,
             )
 
-        def add_squares(n):
-            sums[n] = sum_pool.tile([P, GRID], F32, name="sum")
-            nc.gpsimd.tensor_tensor(out=sums[n][:], in0=diffs[n][:, 0, :], in1=diffs[n][:, 1, :], op=ALU.add)
+        def turn_back(s):
+            r = s // (HALVES * NL)
+            sums[s] = summed.tile([P, BANK], F32, name="sum")
+            for q in range(BANK // P):
+                cols = slice(q * P, (q + 1) * P)
+                block = (s % HALVES) * 2 + q % 2
+                parts = [turned[s][:, cols], b_cols[:, block, r * P : (r + 1) * P]]
+                for w, part in enumerate(parts):
+                    nc.tensor.matmul(
+                        out=sums[s][:, cols],
+                        lhsT=part,
+                        rhs=ident[:],
+                        is_transpose=True,
+                        start=(w == 0),
+                        stop=(w == len(parts) - 1),
+                    )
 
-        def add_child_term(n):
+        def finish(s):
+            n, h = s // HALVES, s % HALVES
             r, i = n // NL, n % NL
-            view = sums[n][:].rearrange("p (s v) -> p s v", v=KU)
-            nc.vector.scalar_tensor_tensor(
-                out=view,
-                in0=view,
-                scalar=c_neg[:, r : r + 1],
-                in1=a_term[r][:, i * T * NL : (i + 1) * T * NL].unsqueeze(2).to_broadcast([P, T * NL, KU]),
-                op0=ALU.mult,
-                op1=ALU.add,
-            )
-            if i == NL - 1 and r + 1 < ROW_TILES:
-                place_child_term(r + 1)
-
-        def add_parent_term(n):
-            r, i = n // NL, n % NL
-            outs[n] = out_pool.tile([P, GRID], F32, name="outt")
+            outs[s] = out_pool.tile([P, HALF], F32, name="outt")
+            first = (i * NL + h * NJ) * T * T
             nc.vector.tensor_tensor(
-                out=outs[n][:].rearrange("p (a t u) -> p a t u", t=T, u=T),
-                in0=sums[n][:].rearrange("p (t a u) -> p a t u", t=T, u=T),
-                in1=b_term[r][:].rearrange("p (a u) -> p a u", u=T).unsqueeze(2).to_broadcast([P, NL * NL, T, T]),
+                out=outs[s][:].rearrange("p (j k t u) -> p j k t u", j=NJ, k=NL, t=T),
+                in0=a_rows[:, r, first : first + NJ * T * T]
+                .rearrange("p (j t u) -> p j t u", j=NJ, t=T)
+                .unsqueeze(2)
+                .to_broadcast([P, NJ, NL, T, T]),
+                in1=sums[s][:].rearrange("p (t j k u) -> p j k t u", t=T, j=NJ, k=NL),
                 op=ALU.add,
             )
-            if i == NL - 1 and r + 1 < ROW_TILES:
-                place_parent_term(r + 1)
+            nc.sync.dma_start(out=out_rows[r * P : (r + 1) * P, i, h * HALF : (h + 1) * HALF], in_=outs[s][:])
 
-        def take_log(n):
-            nc.scalar.activation(out=prods[n][:], in_=prods[n][:], func=FUNC.Ln)
+        ahead = []
+        for b in range(UNITS // BATCH):
+            ahead.extend([("log", s) for s in range(b * BATCH, (b + 1) * BATCH)])
+            ahead.extend([("root", s) for s in range(b * BATCH, (b + 1) * BATCH)])
+        at = {"ahead": 0}
 
-        def finish(n):
-            r, i = n // NL, n % NL
-            nc.vector.scalar_tensor_tensor(
-                out=outs[n][:],
-                in0=prods[n][:],
-                scalar=c_pos[:, r : r + 1],
-                in1=outs[n][:],
-                op0=ALU.mult,
-                op1=ALU.add,
-            )
-            nc.sync.dma_start(out=out_rows[r * P : (r + 1) * P, i, :], in_=outs[n][:])
+        def issue_ahead(count):
+            for kind, s in ahead[at["ahead"] : at["ahead"] + count]:
+                if kind == "log":
+                    take_logs(s)
+                else:
+                    make_roots(s)
+            at["ahead"] = at["ahead"] + count
 
-        def live(n):
-            return 0 <= n < CHUNKS
+        def live(s):
+            return 0 <= s < UNITS
 
-        place_child_term(0)
-        place_parent_term(0)
-        for n in range(ROOT_LEAD):
-            make_roots(n)
-        for step in range(CHUNKS + FINAL_LAG + 1):
-            if live(step + ROOT_LEAD):
-                make_roots(step + ROOT_LEAD)
+        issue_ahead(LEAD)
+        for step in range(UNITS + 3):
+            issue_ahead(2)
+            if live(step):
+                if step > 0 and step % (HALVES * NL) == 0:
+                    place_m2(step // (HALVES * NL))
+                make_diffs(step)
+                square_diffs(step)
             if live(step - 1):
-                make_diffs(step - 1)
-                multiply_roots(step - 1)
+                gather(step - 1)
             if live(step - 2):
-                square_diffs(step - 2)
+                scale_sum(step - 2)
+                turn_back(step - 2)
             if live(step - 3):
-                add_squares(step - 3)
-            if live(step - 4):
-                add_child_term(step - 4)
-            if live(step - 5):
-                add_parent_term(step - 5)
-            if live(step - 2) and (step - 1) % LN_BLOCK == 0:
-                for n in range(step - 1 - LN_BLOCK, step - 1):
-                    take_log(n)
-            if live(step - FINAL_LAG):
-                finish(step - FINAL_LAG)
+                finish(step - 3)

@@ -36,6 +36,8 @@ NJ = NL // HALVES
 HALF = GRID // HALVES
 BATCH = 12
 LEAD = BATCH + 6
+LOGS = BATCH + 7
+EARLY = 8
 
 FLOPS = 2 * ROWS * D * (JKU + 2 * JKU * G)
 
@@ -85,6 +87,8 @@ def tile_chainlveg_pb_kernel(
                     dst[:, q * P : (q + 1) * P], cols[:, first_block + q, r * P : (r + 1) * P], ident[:]
                 )
 
+        early_pool = ctx.enter_context(tc.tile_pool(name="early", bufs=EARLY, reuse_waits="tile"))
+
         def place_m2(r):
             for h in range(2):
                 m2[h] = resident.tile([P, BANK], F32, name="m2_%d" % h)
@@ -102,10 +106,10 @@ def tile_chainlveg_pb_kernel(
             raw["tpv"] = load.tile([P, PASSES, PACK * widths["tpv"]], BF16, name="raw_tpv")
             var_sb = load.tile([P, ROW_TILES, CS], BF16, name="var_sb")
             raw["tpm"] = load.tile([P, PASSES, PACK * widths["tpm"]], BF16, name="raw_tpm")
-            e2_cols = load.tile([P, JKU * G // P, ROWS], F32, name="e2_cols")
             raw["tw"] = load.tile([P, PASSES, PACK * widths["tw"]], BF16, name="raw_tw")
             scale_sb = load.tile([P, ROW_TILES, CS // G], BF16, name="scale_sb")
             c_rows = load.tile([P, ROWS], F32, name="c_rows")
+            e2_cols = load.tile([P, JKU * G // P, ROWS], F32, name="e2_cols")
             nc.vector.memset(rows_bf[:], 0.0)
             nc.scalar.dma_start(out=rows_bf[0:4, :], in_=tw_b.rearrange("(r p) -> r p", p=P))
             nc.scalar.dma_start(out=rows_bf[4:12, :], in_=tpm_b.rearrange("(r p) -> r p", p=P))
@@ -167,24 +171,24 @@ def tile_chainlveg_pb_kernel(
                 codes[name] = quant.tile([P, PASSES, widths[name]], U32, name="codes_" + name, align_bytes=64)
                 scales[name] = quant.tile([P, PASSES, widths[name]], U8, name="scales_" + name, align_bytes=64)
 
-            def quantise_weight(name, scalar_helps):
-                grouped = {}
-                for c in range(PASSES):
-                    grouped[c] = group.tile([P, PACK * JKU * G], BF16, name="grouped", align_bytes=64)
-                    src = raw[name][:, c, :].rearrange("p (t a i) -> p a t i", t=PACK, i=4)
-                    dst = grouped[c][:, 0 : PACK * widths[name]].rearrange("p (a i t) -> p a t i", i=4, t=PACK)
-                    for h in range(widths[name] // PIECE):
-                        runs = slice(h * PIECE // 4, (h + 1) * PIECE // 4)
-                        if scalar_helps and h % 2 == 1:
-                            nc.scalar.copy(out=dst[:, runs], in_=src[:, runs])
-                        else:
-                            nc.vector.tensor_copy(out=dst[:, runs], in_=src[:, runs])
-                for c in range(PASSES):
-                    nc.vector.quantize_mx(
-                        out=codes[name][:, c, :].bitcast(FP8X4),
-                        scales=scales[name][:, c, :],
-                        in_=grouped[c][:, 0 : PACK * widths[name]],
-                    )
+            def regroup(name, c, scalar_helps):
+                grouped = group.tile([P, PACK * JKU * G], BF16, name="grouped", align_bytes=64)
+                src = raw[name][:, c, :].rearrange("p (t n) -> p n t", t=PACK)
+                dst = grouped[:, 0 : PACK * widths[name]].rearrange("p (n t) -> p n t", t=PACK)
+                for h in range(widths[name] // PIECE):
+                    runs = slice(h * PIECE, (h + 1) * PIECE)
+                    if scalar_helps and h % 2 == 1:
+                        nc.scalar.copy(out=dst[:, runs], in_=src[:, runs])
+                    else:
+                        nc.vector.tensor_copy(out=dst[:, runs], in_=src[:, runs])
+                return grouped
+
+            def quantise(name, c, grouped):
+                nc.vector.quantize_mx(
+                    out=codes[name][:, c, :].bitcast(FP8X4),
+                    scales=scales[name][:, c, :],
+                    in_=grouped[:, 0 : PACK * widths[name]],
+                )
 
             def product(name, block):
                 acc = work.tile([P, BANK], F32, name="bank")
@@ -202,21 +206,7 @@ def tile_chainlveg_pb_kernel(
                         )
                 return acc
 
-            quantise_weight("tpv", True)
-            for r in range(ROW_TILES):
-                nc.scalar.activation(out=e1[:, r, :], in_=var_sb[:, r, :], func=FUNC.Exp, scale=2.0)
-            quantise_weight("tpm", False)
-
-            for block in range(JKU * G // P):
-                acc = product("tpv", block)
-                nc.scalar.activation(
-                    out=e2_cols[:, block, :],
-                    in_=acc[:, 0:ROWS],
-                    func=FUNC.Exp,
-                    bias=v_bias2[:, block : block + 1],
-                    scale=2.0,
-                )
-            for r in range(ROW_TILES):
+            def place_e2(r):
                 for h in range(2):
                     back = work.tile([P, BANK], F32, name="bank")
                     to_rows(back, e2_cols, 4 * h, r)
@@ -228,6 +218,26 @@ def tile_chainlveg_pb_kernel(
                         op0=ALU.min,
                         op1=ALU.max,
                     )
+
+            pieces = [regroup("tpv", c, True) for c in range(PASSES)]
+            for c in range(PASSES):
+                quantise("tpv", c, pieces[c])
+            for r in range(ROW_TILES):
+                nc.scalar.activation(out=e1[:, r, :], in_=var_sb[:, r, :], func=FUNC.Exp, scale=2.0)
+            for block in range(JKU * G // P):
+                acc = product("tpv", block)
+                nc.scalar.activation(
+                    out=e2_cols[:, block, :],
+                    in_=acc[:, 0:ROWS],
+                    func=FUNC.Exp,
+                    bias=v_bias2[:, block : block + 1],
+                    scale=2.0,
+                )
+            pieces = [regroup("tpm", 0, False)]
+            place_e2(0)
+            pieces.append(regroup("tpm", 1, False))
+            for c in range(PASSES):
+                quantise("tpm", c, pieces[c])
 
             for block in range(JKU * G // P):
                 acc = product("tpm", block)
@@ -242,7 +252,9 @@ def tile_chainlveg_pb_kernel(
             nc.vector.tensor_scalar_max(out=m2_cols[:], in0=m2_cols[:], scalar1=-1.0)
             place_m2(0)
 
-            quantise_weight("tw", False)
+            pieces = [regroup("tw", c, False) for c in range(PASSES)]
+            for c in range(PASSES):
+                quantise("tw", c, pieces[c])
             c_bank = work.tile([P, BANK], F32, name="bank")
             for r in range(ROW_TILES):
                 nc.tensor.transpose(c_bank[:, r * P : (r + 1) * P], c_pos[:, r : r + 1].to_broadcast([P, P]), ident[:])
@@ -265,8 +277,10 @@ def tile_chainlveg_pb_kernel(
                     in0=scale_sb[:, r, :].unsqueeze(2).to_broadcast([P, JKU, T]),
                     scalar1=mask_h[:, r : r + 1],
                 )
+            for r in range(1, ROW_TILES):
+                place_e2(r)
 
-        logs_pool = ctx.enter_context(tc.tile_pool(name="logs", bufs=BATCH + 7, reuse_waits="tile"))
+        logs_pool = ctx.enter_context(tc.tile_pool(name="logs", bufs=LOGS - EARLY, reuse_waits="tile"))
         roots_pool = ctx.enter_context(tc.tile_pool(name="roots", bufs=BATCH, reuse_waits="tile"))
         diff_pool = ctx.enter_context(tc.tile_pool(name="diff", bufs=4, reuse_waits="tile"))
         turn_pool = ctx.enter_context(tc.tile_pool(name="turn", bufs=3, reuse_waits="tile"))
@@ -290,7 +304,7 @@ def tile_chainlveg_pb_kernel(
 
         def take_logs(s):
             r = s // (HALVES * NL)
-            logs[s] = logs_pool.tile([P, G, HALF], F32, name="log")
+            logs[s] = (early_pool if s % LOGS < EARLY else logs_pool).tile([P, G, HALF], F32, name="log")
             for g, j, col, where in unit_slots(s):
                 nc.scalar.activation(
                     out=logs[s][:, g, where],

@@ -34,10 +34,12 @@ HALVES = 2
 UNITS = CHUNKS * HALVES
 NJ = NL // HALVES
 HALF = GRID // HALVES
-BATCH = 12
+BATCH = 16
+BATCHES = [BATCH] * 5 + [12, 4]
 LEAD = BATCH + 6
-LOGS = BATCH + 7
+LOGS = BATCH + 6
 EARLY = 8
+WIDE_EVERY = 4
 
 FLOPS = 2 * ROWS * D * (JKU + 2 * JKU * G)
 
@@ -281,7 +283,7 @@ def tile_chainlveg_pb_kernel(
                 place_e2(r)
 
         logs_pool = ctx.enter_context(tc.tile_pool(name="logs", bufs=LOGS - EARLY, reuse_waits="tile"))
-        roots_pool = ctx.enter_context(tc.tile_pool(name="roots", bufs=BATCH, reuse_waits="tile"))
+        roots_pool = ctx.enter_context(tc.tile_pool(name="roots", bufs=BATCH - 3, reuse_waits="tile"))
         diff_pool = ctx.enter_context(tc.tile_pool(name="diff", bufs=4, reuse_waits="tile"))
         turn_pool = ctx.enter_context(tc.tile_pool(name="turn", bufs=3, reuse_waits="tile"))
         out_pool = ctx.enter_context(tc.tile_pool(name="outp", bufs=4, reuse_waits="tile"))
@@ -305,6 +307,24 @@ def tile_chainlveg_pb_kernel(
         def take_logs(s):
             r = s // (HALVES * NL)
             logs[s] = (early_pool if s % LOGS < EARLY else logs_pool).tile([P, G, HALF], F32, name="log")
+            if s % WIDE_EVERY == WIDE_EVERY - 1:
+                i, h = (s // HALVES) % NL, s % HALVES
+                first = (i * NL + h * NJ) * T * G
+                for g in range(G):
+                    nc.gpsimd.tensor_tensor(
+                        out=logs[s][:, g, :].rearrange("p (t j v) -> p t j v", t=T, j=NJ),
+                        in0=e2[:, r, g, h * NJ * KU : (h + 1) * NJ * KU]
+                        .rearrange("p (j v) -> p j v", j=NJ)
+                        .unsqueeze(1)
+                        .to_broadcast([P, T, NJ, KU]),
+                        in1=e1[:, r, first : first + NJ * T * G]
+                        .rearrange("p (j t g) -> p g t j", t=T, g=G)[:, g]
+                        .unsqueeze(3)
+                        .to_broadcast([P, T, NJ, KU]),
+                        op=ALU.add,
+                    )
+                nc.scalar.activation(out=logs[s][:], in_=logs[s][:], func=FUNC.Ln)
+                return
             for g, j, col, where in unit_slots(s):
                 nc.scalar.activation(
                     out=logs[s][:, g, where],
@@ -393,10 +413,12 @@ def tile_chainlveg_pb_kernel(
             )
             nc.sync.dma_start(out=out_rows[r * P : (r + 1) * P, i, h * HALF : (h + 1) * HALF], in_=outs[s][:])
 
+        assert sum(BATCHES) == UNITS
         ahead = []
-        for b in range(UNITS // BATCH):
-            ahead.extend([("log", s) for s in range(b * BATCH, (b + 1) * BATCH)])
-            ahead.extend([("root", s) for s in range(b * BATCH, (b + 1) * BATCH)])
+        for b, size in enumerate(BATCHES):
+            first = sum(BATCHES[:b])
+            ahead.extend([("log", s) for s in range(first, first + size)])
+            ahead.extend([("root", s) for s in range(first, first + size)])
         at = {"ahead": 0}
 
         def issue_ahead(count):

@@ -35,11 +35,10 @@ UNITS = CHUNKS * HALVES
 NJ = NL // HALVES
 HALF = GRID // HALVES
 BATCH = 16
-BATCHES = [BATCH] * 5 + [12, 4]
-LEAD = BATCH + 6
+BATCHES = [12] + [BATCH] * 4 + [12, 8]
+LEAD = BATCHES[0] + 8
 LOGS = BATCH + 6
 EARLY = 8
-WIDE_EVERY = 4
 
 FLOPS = 2 * ROWS * D * (JKU + 2 * JKU * G)
 
@@ -286,7 +285,7 @@ def tile_chainlveg_pb_kernel(
         roots_pool = ctx.enter_context(tc.tile_pool(name="roots", bufs=BATCH - 3, reuse_waits="tile"))
         diff_pool = ctx.enter_context(tc.tile_pool(name="diff", bufs=4, reuse_waits="tile"))
         turn_pool = ctx.enter_context(tc.tile_pool(name="turn", bufs=3, reuse_waits="tile"))
-        out_pool = ctx.enter_context(tc.tile_pool(name="outp", bufs=4, reuse_waits="tile"))
+        out_pool = ctx.enter_context(tc.tile_pool(name="outp", bufs=6, reuse_waits="tile"))
         logs = {}
         roots = {}
         diffs = {}
@@ -307,7 +306,7 @@ def tile_chainlveg_pb_kernel(
         def take_logs(s):
             r = s // (HALVES * NL)
             logs[s] = (early_pool if s % LOGS < EARLY else logs_pool).tile([P, G, HALF], F32, name="log")
-            if s % WIDE_EVERY == WIDE_EVERY - 1:
+            if s < BATCHES[0] and s % 2 == 1:
                 i, h = (s // HALVES) % NL, s % HALVES
                 first = (i * NL + h * NJ) * T * G
                 for g in range(G):

@@ -38,7 +38,7 @@ BATCH = 16
 BATCHES = [12] + [BATCH] * 4 + [12, 8]
 LEAD = BATCHES[0] + 8
 LOGS = BATCH + 6
-EARLY = 8
+EARLY = BATCHES[0]
 
 FLOPS = 2 * ROWS * D * (JKU + 2 * JKU * G)
 
@@ -136,10 +136,10 @@ def tile_chainlveg_pb_kernel(
             load_weight("tw")
             nc.sync.dma_start(out=scale_sb[:], in_=scale_rows)
 
-            x_group = quant.tile([P, ROW_TILES * PASSES * P * PACK], BF16, name="x_group", align_bytes=64)
+            x_group = group.tile([P, PACK * JKU * G], BF16, name="grouped", align_bytes=64)
             x_codes = quant.tile([P, ROW_TILES, PASSES, P], U32, name="x_codes", align_bytes=64)
             x_scales = quant.tile([P, ROW_TILES, PASSES, P], U8, name="x_scales", align_bytes=64)
-            x_group_words = x_group[:].bitcast(F32).rearrange(
+            x_group_words = x_group[:, 0 : ROW_TILES * PASSES * P * PACK].bitcast(F32).rearrange(
                 "p (r c m u) -> p r c m u", r=ROW_TILES, c=PASSES, m=P, u=2
             )
             for r in range(ROW_TILES):

import math
from contextlib import ExitStack

import concourse.mybir as mybir
from concourse.masks import make_identity

F32 = mybir.dt.float32
BF16 = mybir.dt.bfloat16
U32 = mybir.dt.uint32
U8 = mybir.dt.uint8
FP8X4 = mybir.dt.float8_e4m3fn_x4
ALU = mybir.AluOpType
FUNC = mybir.ActivationFunctionType

P = 128
ROWS = 384
ROW_TILES = ROWS // P
D = 1024
PACK = 4
K_PASS = P * PACK
PASSES = D // K_PASS
NL = 16
T = 2
G = 2
KU = NL * T
JKU = NL * KU
CS = NL * NL * T * G
GRID = NL * NL * T * T
BANK = 512
PIECE = 512
LOG_2PI = math.log(2.0 * math.pi)
CHUNKS = ROW_TILES * NL
HALVES = 2
UNITS = CHUNKS * HALVES
NJ = NL // HALVES
HALF = GRID // HALVES
BATCH = 16
BATCHES = [12] + [BATCH] * 4 + [12, 8]
LEAD = BATCHES[0] + 8
LOGS = BATCH + 6
EARLY = BATCHES[0]

FLOPS = 2 * ROWS * D * (JKU + 2 * JKU * G)


def tile_chainlveg_pb_kernel(
    tc, x_next, cs_scale, cs_mu, cs_var, mask_here, mask_next, tw_w, tw_b, tpm_w, tpm_b, tpv_w, tpv_b, out
):
    nc = tc.nc
    weights = {"tpv": tpv_w, "tpm": tpm_w, "tw": tw_w}
    widths = {"tpv": JKU * G, "tpm": JKU * G, "tw": JKU}

    x_rows = x_next.rearrange("b q k -> (b q) k").rearrange("(r p) k -> p r k", p=P)
    var_rows = cs_var.rearrange("b q i j t e g -> (b q) (i j t e g)").rearrange("(r p) f -> p r f", p=P)
    mu_rows = cs_mu.rearrange("b q i j t e g -> (b q) (i j t e g)").rearrange("(r p) f -> p r f", p=P)
    scale_rows = cs_scale.rearrange("b q i j t e -> (b q) (i j t e)").rearrange("(r p) f -> p r f", p=P)
    out_rows = out.rearrange("b q i j k t e u -> (b q) i (j k t e u)")

    with ExitStack() as ctx:
        ctx.enter_context(tc.manual_schedule())
        keep = ctx.enter_context(tc.tile_pool(name="keep", bufs=1))
        work = ctx.enter_context(tc.psum_pool(name="work", bufs=4))
        summed = ctx.enter_context(tc.psum_pool(name="summed", bufs=2))
        resident = ctx.enter_context(tc.psum_pool(name="resident", bufs=1))

        ident = keep.tile([P, P], F32, name="ident")
        e1 = keep.tile([P, ROW_TILES, CS], F32, name="e1")
        m1 = keep.tile([P, ROW_TILES, CS], BF16, name="m1")
        e2 = keep.tile([P, ROW_TILES, G, JKU], F32, name="e2")
        a_rows = keep.tile([P, ROW_TILES, JKU * T], F32, name="a_rows")
        b_cols = keep.tile([P, JKU // P, ROWS], F32, name="b_cols")
        ch_rows = keep.tile([P, ROWS], F32, name="ch_rows")
        m2_cols = keep.tile([P, JKU * G // P, ROWS], F32, name="m2_cols")
        small = keep.tile([P, 32], F32, name="small")
        tw_bias = keep.tile([P, 4], F32, name="tw_bias")
        v_bias2 = keep.tile([P, 8], F32, name="v_bias2")
        c_pos = keep.tile([P, ROW_TILES], F32, name="c_pos")
        m_bias = small[:, 4:12]
        mask_h = small[:, 20:23]
        mask_n = small[:, 23:26]
        m2 = {}

        make_identity(nc, ident[:])

        def to_rows(dst, cols, first_block, r):
            for q in range(BANK // P):
                nc.tensor.transpose(
                    dst[:, q * P : (q + 1) * P], cols[:, first_block + q, r * P : (r + 1) * P], ident[:]
                )

        early_pool = ctx.enter_context(tc.tile_pool(name="early", bufs=EARLY, reuse_waits="tile"))

        def place_m2(r):
            for h in range(2):
                m2[h] = resident.tile([P, BANK], F32, name="m2_%d" % h)
                to_rows(m2[h], m2_cols, 4 * h, r)

        with ExitStack() as pro:
            load = pro.enter_context(tc.tile_pool(name="load", bufs=1))
            group = pro.enter_context(tc.tile_pool(name="group", bufs=3))
            quant = pro.enter_context(tc.tile_pool(name="quant", bufs=1))

            rows_bf = load.tile([P, P], BF16, name="rows_bf")
            rows_f = load.tile([P, P], F32, name="rows_f")
            x_sb = load.tile([P, ROW_TILES, D], BF16, name="x_sb")
            raw = {}
            raw["tpv"] = load.tile([P, PASSES, PACK * widths["tpv"]], BF16, name="raw_tpv")
            var_sb = load.tile([P, ROW_TILES, CS], BF16, name="var_sb")
            raw["tpm"] = load.tile([P, PASSES, PACK * widths["tpm"]], BF16, name="raw_tpm")
            raw["tw"] = load.tile([P, PASSES, PACK * widths["tw"]], BF16, name="raw_tw")
            scale_sb = load.tile([P, ROW_TILES, CS // G], BF16, name="scale_sb")
            c_rows = load.tile([P, ROWS], F32, name="c_rows")
            e2_cols = load.tile([P, JKU * G // P, ROWS], F32, name="e2_cols")
            nc.vector.memset(rows_bf[:], 0.0)
            nc.scalar.dma_start(out=rows_bf[0:4, :], in_=tw_b.rearrange("(r p) -> r p", p=P))
            nc.scalar.dma_start(out=rows_bf[4:12, :], in_=tpm_b.rearrange("(r p) -> r p", p=P))
            nc.scalar.dma_start(out=rows_bf[12:20, :], in_=tpv_b.rearrange("(r p) -> r p", p=P))
            nc.scalar.dma_start(
                out=rows_bf[20:23, :], in_=mask_here.rearrange("b q -> (b q)").rearrange("(r p) -> r p", p=P)
            )
            nc.scalar.dma_start(
                out=rows_bf[23:26, :], in_=mask_next.rearrange("b q -> (b q)").rearrange("(r p) -> r p", p=P)
            )

            nc.sync.dma_start(out=x_sb[:], in_=x_rows)

            def load_weight(name):
                view = weights[name].rearrange("(c u p e) n -> c p u (e n)", c=PASSES, u=2, p=P, e=2)
                for c in range(PASSES):
                    nc.sync.dma_start(out=raw[name][:, c, :].rearrange("p (u f) -> p u f", u=2), in_=view[c])

            load_weight("tpv")
            nc.sync.dma_start(out=var_sb[:], in_=var_rows)
            load_weight("tpm")
            nc.sync.dma_start(out=m1[:], in_=mu_rows)
            load_weight("tw")
            nc.sync.dma_start(out=scale_sb[:], in_=scale_rows)

            x_group = group.tile([P, PACK * JKU * G], BF16, name="grouped", align_bytes=64)
            x_codes = quant.tile([P, ROW_TILES, PASSES, P], U32, name="x_codes", align_bytes=64)
            x_scales = quant.tile([P, ROW_TILES, PASSES, P], U8, name="x_scales", align_bytes=64)
            x_group_words = x_group[:, 0 : ROW_TILES * PASSES * P * PACK].bitcast(F32).rearrange(
                "p (r c m u) -> p r c m u", r=ROW_TILES, c=PASSES, m=P, u=2
            )
            for r in range(ROW_TILES):
                x_words = x_sb[:, r, :].bitcast(F32)
                xt = work.tile([P, BANK], F32, name="bank")
                for cu in range(PASSES * 2):
                    nc.tensor.transpose(xt[:, cu * P : (cu + 1) * P], x_words[:, cu * P : (cu + 1) * P], ident[:])
                nc.vector.tensor_copy(
                    out=x_group_words[:, r], in_=xt[:].rearrange("p (c u m) -> p c m u", c=PASSES, u=2)
                )
            nc.vector.tensor_copy(out=rows_f[:], in_=rows_bf[:])
            small_ps = work.tile([P, BANK], F32, name="bank")
            nc.tensor.transpose(small_ps[:, 0:P], rows_f[:], ident[:])
            nc.vector.tensor_copy(out=small[:], in_=small_ps[:, 0:32])
            nc.vector.tensor_scalar_add(out=tw_bias[:], in0=small[:, 0:4], scalar1=-LOG_2PI)
            nc.vector.tensor_scalar_mul(out=v_bias2[:], in0=small[:, 12:20], scalar1=2.0)
            nc.vector.tensor_tensor(out=c_pos[:], in0=mask_h, in1=mask_n, op=ALU.mult)

            per_tile = PASSES * P * PACK
            for r in range(ROW_TILES):
                nc.vector.quantize_mx(
                    out=x_codes[:, r].rearrange("p c m -> p (c m)").bitcast(FP8X4),
                    scales=x_scales[:, r].rearrange("p c m -> p (c m)"),
                    in_=x_group[:, r * per_tile : (r + 1) * per_tile],
                )

            codes = {}
            scales = {}
            for name in ("tpv", "tpm", "tw"):
                codes[name] = quant.tile([P, PASSES, widths[name]], U32, name="codes_" + name, align_bytes=64)
                scales[name] = quant.tile([P, PASSES, widths[name]], U8, name="scales_" + name, align_bytes=64)

            def regroup(name, c, scalar_helps):
                grouped = group.tile([P, PACK * JKU * G], BF16, name="grouped", align_bytes=64)
                src = raw[name][:, c, :].rearrange("p (t n) -> p n t", t=PACK)
                dst = grouped[:, 0 : PACK * widths[name]].rearrange("p (n t) -> p n t", t=PACK)
                for h in range(widths[name] // PIECE):
                    runs = slice(h * PIECE, (h + 1) * PIECE)
                    if scalar_helps and h % 2 == 1:
                        nc.scalar.copy(out=dst[:, runs], in_=src[:, runs])
                    else:
                        nc.vector.tensor_copy(out=dst[:, runs], in_=src[:, runs])
                return grouped

            def quantise(name, c, grouped):
                nc.vector.quantize_mx(
                    out=codes[name][:, c, :].bitcast(FP8X4),
                    scales=scales[name][:, c, :],
                    in_=grouped[:, 0 : PACK * widths[name]],
                )

            def product(name, block):
                acc = work.tile([P, BANK], F32, name="bank")
                cols = slice(block * P, (block + 1) * P)
                for r in range(ROW_TILES):
                    for c in range(PASSES):
                        nc.tensor.matmul_mx(
                            out=acc[:, r * P : (r + 1) * P],
                            lhsT=codes[name][:, c, cols].bitcast(FP8X4),
                            lhsT_scale=scales[name][:, c, cols],
                            rhs=x_codes[:, r, c, :].bitcast(FP8X4),
                            rhs_scale=x_scales[:, r, c, :],
                            start=(c == 0),
                            stop=(c == PASSES - 1),
                        )
                return acc

            def place_e2(r):
                for h in range(2):
                    back = work.tile([P, BANK], F32, name="bank")
                    to_rows(back, e2_cols, 4 * h, r)
                    nc.vector.tensor_scalar(
                        out=e2[:, r, :, h * BANK // G : (h + 1) * BANK // G],
                        in0=back[:].rearrange("p (a g) -> p g a", g=G),
                        scalar1=math.exp(2.0),
                        scalar2=math.exp(-2.0),
                        op0=ALU.min,
                        op1=ALU.max,
                    )

            pieces = [regroup("tpv", c, True) for c in range(PASSES)]
            for c in range(PASSES):
                quantise("tpv", c, pieces[c])
            for r in range(ROW_TILES):
                nc.scalar.activation(out=e1[:, r, :], in_=var_sb[:, r, :], func=FUNC.Exp, scale=2.0)
            for block in range(JKU * G // P):
                acc = product("tpv", block)
                nc.scalar.activation(
                    out=e2_cols[:, block, :],
                    in_=acc[:, 0:ROWS],
                    func=FUNC.Exp,
                    bias=v_bias2[:, block : block + 1],
                    scale=2.0,
                )
            pieces = [regroup("tpm", 0, False)]
            place_e2(0)
            pieces.append(regroup("tpm", 1, False))
            for c in range(PASSES):
                quantise("tpm", c, pieces[c])

            for block in range(JKU * G // P):
                acc = product("tpm", block)
                nc.vector.tensor_scalar(
                    out=m2_cols[:, block, :],
                    in0=acc[:, 0:ROWS],
                    scalar1=m_bias[:, block : block + 1],
                    scalar2=1.0,
                    op0=ALU.add,
                    op1=ALU.min,
                )
            nc.vector.tensor_scalar_max(out=m2_cols[:], in0=m2_cols[:], scalar1=-1.0)
            place_m2(0)

            pieces = [regroup("tw", c, False) for c in range(PASSES)]
            for c in range(PASSES):
                quantise("tw", c, pieces[c])
            c_bank = work.tile([P, BANK], F32, name="bank")
            for r in range(ROW_TILES):
                nc.tensor.transpose(c_bank[:, r * P : (r + 1) * P], c_pos[:, r : r + 1].to_broadcast([P, P]), ident[:])
            nc.vector.tensor_copy(out=c_rows[:], in_=c_bank[:, 0:ROWS])
            nc.vector.tensor_scalar_mul(out=ch_rows[:], in0=c_bank[:, 0:ROWS], scalar1=-0.5)
            for block in range(JKU // P):
                acc = product("tw", block)
                nc.vector.scalar_tensor_tensor(
                    out=b_cols[:, block, :],
                    in0=acc[:, 0:ROWS],
                    scalar=tw_bias[:, block : block + 1],
                    in1=c_rows[:],
                    op0=ALU.add,
                    op1=ALU.mult,
                )

            for r in range(ROW_TILES):
                nc.vector.tensor_scalar_mul(
                    out=a_rows[:, r, :].rearrange("p (s u) -> p s u", u=T),
                    in0=scale_sb[:, r, :].unsqueeze(2).to_broadcast([P, JKU, T]),
                    scalar1=mask_h[:, r : r + 1],
                )
            for r in range(1, ROW_TILES):
                place_e2(r)

        logs_pool = ctx.enter_context(tc.tile_pool(name="logs", bufs=LOGS - EARLY, reuse_waits="tile"))
        roots_pool = ctx.enter_context(tc.tile_pool(name="roots", bufs=BATCH - 3, reuse_waits="tile"))
        diff_pool = ctx.enter_context(tc.tile_pool(name="diff", bufs=4, reuse_waits="tile"))
        turn_pool = ctx.enter_context(tc.tile_pool(name="turn", bufs=3, reuse_waits="tile"))
        out_pool = ctx.enter_context(tc.tile_pool(name="outp", bufs=6, reuse_waits="tile"))
        logs = {}
        roots = {}
        diffs = {}
        gathered = {}
        turned = {}
        sums = {}
        outs = {}

        def unit_slots(s):
            i, h = (s // HALVES) % NL, s % HALVES
            return [
                (g, j, ((i * NL + j) * T + t) * G + g, slice((t * NJ + j % NJ) * KU, (t * NJ + j % NJ + 1) * KU))
                for g in range(G)
                for t in range(T)
                for j in range(h * NJ, (h + 1) * NJ)
            ]

        def take_logs(s):
            r = s // (HALVES * NL)
            logs[s] = (early_pool if s % LOGS < EARLY else logs_pool).tile([P, G, HALF], F32, name="log")
            if s < BATCHES[0] and s % 2 == 1:
                i, h = (s // HALVES) % NL, s % HALVES
                first = (i * NL + h * NJ) * T * G
                for g in range(G):
                    nc.gpsimd.tensor_tensor(
                        out=logs[s][:, g, :].rearrange("p (t j v) -> p t j v", t=T, j=NJ),
                        in0=e2[:, r, g, h * NJ * KU : (h + 1) * NJ * KU]
                        .rearrange("p (j v) -> p j v", j=NJ)
                        .unsqueeze(1)
                        .to_broadcast([P, T, NJ, KU]),
                        in1=e1[:, r, first : first + NJ * T * G]
                        .rearrange("p (j t g) -> p g t j", t=T, g=G)[:, g]
                        .unsqueeze(3)
                        .to_broadcast([P, T, NJ, KU]),
                        op=ALU.add,
                    )
                nc.scalar.activation(out=logs[s][:], in_=logs[s][:], func=FUNC.Ln)
                return
            for g, j, col, where in unit_slots(s):
                nc.scalar.activation(
                    out=logs[s][:, g, where],
                    in_=e2[:, r, g, j * KU : (j + 1) * KU],
                    func=FUNC.Ln,
                    bias=e1[:, r, col : col + 1],
                    scale=1.0,
                )

        def make_roots(s):
            roots[s] = roots_pool.tile([P, G, HALF], F32, name="root")
            nc.scalar.activation(out=roots[s][:], in_=logs[s][:], func=FUNC.Exp, scale=-0.5)

        def make_diffs(s):
            r = s // (HALVES * NL)
            diffs[s] = diff_pool.tile([P, G, HALF], F32, name="diff")
            for g, j, col, where in unit_slots(s):
                m2_view = m2[j // 8][:].rearrange("p (j a g) -> p j g a", j=8, g=G)
                nc.vector.scalar_tensor_tensor(
                    out=diffs[s][:, g, where],
                    in0=m2_view[:, j % 8, g, :],
                    scalar=m1[:, r, col : col + 1],
                    in1=roots[s][:, g, where],
                    op0=ALU.subtract,
                    op1=ALU.mult,
                )

        def square_diffs(s):
            nc.gpsimd.tensor_tensor(out=diffs[s][:], in0=diffs[s][:], in1=diffs[s][:], op=ALU.mult)

        def gather(s):
            gathered[s] = work.tile([P, BANK], F32, name="bank")
            for q in range(BANK // P):
                cols = slice(q * P, (q + 1) * P)
                parts = [logs[s][:, 0, cols], logs[s][:, 1, cols], diffs[s][:, 0, cols], diffs[s][:, 1, cols]]
                for w, part in enumerate(parts):
                    nc.tensor.matmul(
                        out=gathered[s][:, cols],
                        lhsT=part,
                        rhs=ident[:],
                        is_transpose=True,
                        start=(w == 0),
                        stop=(w == len(parts) - 1),
                    )

        def scale_sum(s):
            r = s // (HALVES * NL)
            turned[s] = turn_pool.tile([P, HALF], F32, name="turned")
            nc.vector.tensor_tensor(
                out=turned[s][:].rearrange("p (q m) -> p q m", m=P),
                in0=ch_rows[:, r * P : (r + 1) * P].unsqueeze(1).to_broadcast([P, BANK // P, P]),
                in1=gathered[s][:].rearrange("p (q m) -> p q m", m=P),
                op=ALU.mult,
            )

        def turn_back(s):
            r = s // (HALVES * NL)
            sums[s] = summed.tile([P, BANK], F32, name="sum")
            for q in range(BANK // P):
                cols = slice(q * P, (q + 1) * P)
                block = (s % HALVES) * 2 + q % 2
                parts = [turned[s][:, cols], b_cols[:, block, r * P : (r + 1) * P]]
                for w, part in enumerate(parts):
                    nc.tensor.matmul(
                        out=sums[s][:, cols],
                        lhsT=part,
                        rhs=ident[:],
                        is_transpose=True,
                        start=(w == 0),
                        stop=(w == len(parts) - 1),
                    )

        def finish(s):
            n, h = s // HALVES, s % HALVES
            r, i = n // NL, n % NL
            outs[s] = out_pool.tile([P, HALF], F32, name="outt")
            first = (i * NL + h * NJ) * T * T
            nc.vector.tensor_tensor(
                out=outs[s][:].rearrange("p (j k t u) -> p j k t u", j=NJ, k=NL, t=T),
                in0=a_rows[:, r, first : first + NJ * T * T]
                .rearrange("p (j t u) -> p j t u", j=NJ, t=T)
                .unsqueeze(2)
                .to_broadcast([P, NJ, NL, T, T]),
                in1=sums[s][:].rearrange("p (t j k u) -> p j k t u", t=T, j=NJ, k=NL),
                op=ALU.add,
            )
            nc.sync.dma_start(out=out_rows[r * P : (r + 1) * P, i, h * HALF : (h + 1) * HALF], in_=outs[s][:])

        assert sum(BATCHES) == UNITS
        ahead = []
        for b, size in enumerate(BATCHES):
            first = sum(BATCHES[:b])
            ahead.extend([("log", s) for s in range(first, first + size)])
            ahead.extend([("root", s) for s in range(first, first + size)])
        at = {"ahead": 0}

        def issue_ahead(count):
            for kind, s in ahead[at["ahead"] : at["ahead"] + count]:
                if kind == "log":
                    take_logs(s)
                else:
                    make_roots(s)
            at["ahead"] = at["ahead"] + count

        def live(s):
            return 0 <= s < UNITS

        issue_ahead(LEAD)
        for step in range(UNITS + 3):
            issue_ahead(2)
            if live(step):
                if step > 0 and step % (HALVES * NL) == 0:
                    place_m2(step // (HALVES * NL))
                make_diffs(step)
                square_diffs(step)
            if live(step - 1):
                gather(step - 1)
            if live(step - 2):
                scale_sum(step - 2)
                turn_back(step - 2)
            if live(step - 3):
                finish(step - 3)
